import numpy as np
import ml_dtypes


def mxq(x, axis, fmt="e4m3"):
    dtype, down = {"e4m3": (ml_dtypes.float8_e4m3fn, 7), "e5m2": (ml_dtypes.float8_e5m2, 14)}[fmt]
    v = np.moveaxis(np.asarray(x, np.float32).astype(ml_dtypes.bfloat16).astype(np.float64), axis, -1)
    blocks = v.reshape(v.shape[:-1] + (-1, 32))
    amax = np.abs(blocks).max(-1, keepdims=True)
    byte = np.maximum(np.where(amax > 0, np.frexp(amax)[1] - 1 + 127, 0) - down, 1)
    scale = np.exp2(byte - 127.0)
    codes = (blocks / scale).astype(np.float32).astype(dtype).astype(np.float64)
    return np.moveaxis((codes * scale).reshape(v.shape), -1, axis)


WIDE = False


def mx_kscale(k):
    if not WIDE:
        return np.ones(k)
    levels = np.array([10, -10, 5, -5, 0])
    if k % 512:
        return np.exp2(np.random.permutation(np.resize(levels, k // 32))).repeat(32)
    a = np.empty((k // 512, 16))
    for p in range(k // 512):
        a[p, :8] = np.random.permutation(np.resize(levels, 8))
        for g in range(8):
            far = levels[np.abs(levels - a[p, g]) >= 10]
            a[p, g + 8] = far[np.random.randint(len(far))]
    return np.exp2(a.ravel()).repeat(32)


BF16 = ml_dtypes.bfloat16


def bf(x):
    return np.asarray(x, np.float32).astype(BF16)


def f64(x):
    return np.asarray(x).astype(np.float64)


B, C, HD, F, G, O = 128, 8, 8, 1024, 512, 128
N = C * HD


def draw0():
    s, t = mx_kscale(F), mx_kscale(G)
    return {
        "x": bf(np.random.standard_normal((B, C, HD, F)) * s),
        "W1g": bf(np.random.standard_normal((G, F)) * 0.7 * np.sqrt(N / F) / s * t[:, None]),
        "b1g": bf(np.random.standard_normal(G) * 0.2 * t),
        "W2g": bf(np.random.standard_normal((O, G)) * 1.5 / np.sqrt(G) / t),
        "b2g": bf(np.random.standard_normal(O) * 0.2),
    }


def core(x, W1g, b1g, W2g, b2g):
    xn = f64(x).reshape(B * N, F)
    y = mxq(xn, 1, "e4m3") @ mxq(f64(W1g), 1, "e4m3").T
    m1 = np.maximum(y.reshape(B, N, G).sum(1) / N + f64(b1g), 0.0)
    m2 = np.maximum((mxq(m1, 1, "e4m3") @ mxq(f64(W2g), 1, "e4m3").T) + f64(b2g), 0.0)
    return np.broadcast_to(m2[:, None, :], (B, N, O)).copy()


def e4m3fn_bytes(y):
    return np.clip(np.asarray(y, np.float64), -448.0, 448.0).astype(np.float32).astype(ml_dtypes.float8_e4m3fn).view(np.uint8)


def e4m3fn_values(b):
    return np.asarray(b, np.uint8).view(ml_dtypes.float8_e4m3fn).astype(np.float64)


def setup_inputs():
    d = draw0()
    x0 = np.asarray(d['x']).astype(np.float64)
    s = (np.max(np.abs(x0), axis=(0, 1, 2), keepdims=True) / 448.0).astype(np.float32)
    out = {}
    for k, v in d.items():
        if k == 'x':
            out['x_bytes'] = e4m3fn_bytes(x0 / s.astype(np.float64))
            out['x_scale'] = s
        else:
            out[k] = v
    return out


def reference(x_bytes, x_scale, W1g, b1g, W2g, b2g):
    return core(e4m3fn_values(x_bytes) * x_scale.astype(np.float64), W1g, b1g, W2g, b2g)

@@ -1,0 +1,280 @@
+from contextlib import ExitStack
+
+import concourse.mybir as mybir
+from concourse.masks import make_identity
+
+GRAPHS, NODES, F, G, O = 128, 64, 1024, 512, 128
+FLOPS = 2 * GRAPHS * NODES * F * G + 2 * GRAPHS * G * O
+
+F32 = mybir.dt.float32
+BF16 = mybir.dt.bfloat16
+U32 = mybir.dt.uint32
+U8 = mybir.dt.uint8
+FP8 = mybir.dt.float8_e4m3fn
+FP8X4 = mybir.dt.float8_e4m3fn_x4
+MULT = mybir.AluOpType.mult
+ADD = mybir.AluOpType.add
+MAX = mybir.AluOpType.max
+RELU = mybir.ActivationFunctionType.Relu
+
+P = 128
+PACK = 4
+PASSES = F // (P * PACK)
+BATCHES = 4
+BG = GRAPHS // BATCHES
+H = P // BG
+SLOTS = NODES // H
+RUN = 4
+GROUPS = BATCHES * SLOTS // RUN
+GPB = SLOTS // RUN
+REPS = 4
+PATHS = ["CCCC"] + ["ECCC"] * (GROUPS - 1)
+
+
+def tile_gcn_pa_t_kernel(tc, x_bytes, x_scale, W1g, b1g, W2g, b2g, out):
+    nc = tc.nc
+    x_view = x_bytes.rearrange("(q b) (h c) d f -> q (b h) (c d f)", q=BATCHES, h=H)
+    out_view = out.rearrange("(q b) (h s) o -> q (b h) (s o)", q=BATCHES, h=H)
+    scale_row = x_scale.rearrange("a b c f -> (a b c f)")
+
+    with ExitStack() as ctx:
+        const = ctx.enter_context(tc.tile_pool(name="const", bufs=1))
+        bytes_pool = ctx.enter_context(tc.tile_pool(name="bytes_pool", bufs=4))
+        wide_pool = ctx.enter_context(tc.tile_pool(name="wide_pool", bufs=12))
+        scaled_pool = ctx.enter_context(tc.tile_pool(name="scaled_pool", bufs=3))
+        grouped_pool = ctx.enter_context(tc.tile_pool(name="grouped_pool", bufs=4))
+        code_pool = ctx.enter_context(tc.tile_pool(name="code_pool", bufs=5))
+        work = ctx.enter_context(tc.tile_pool(name="work", bufs=2))
+        turn_psum = ctx.enter_context(tc.psum_pool(name="turn_psum", bufs=5))
+        acc_psum = ctx.enter_context(tc.psum_pool(name="acc_psum", bufs=2))
+        small_psum = ctx.enter_context(tc.psum_pool(name="small_psum", bufs=1))
+
+        ident = const.tile([P, P], F32, name="ident")
+        scale_t = const.tile([P, PASSES, PACK], F32, name="scale_t")
+        scale_nat = const.tile([P, F], F32, name="scale_nat")
+        w1 = const.tile([P, PACK, F], BF16, name="w1")
+        w1_grouped = const.tile([P, PASSES, G, PACK], BF16, name="w1_grouped", align_bytes=64)
+        w1_codes = const.tile([P, PASSES, G], U32, name="w1_codes", align_bytes=64)
+        w1_scales = const.tile([P, PASSES, G], U8, name="w1_scales", align_bytes=64)
+        w2 = const.tile([P, G], BF16, name="w2")
+        w2_grouped = const.tile([P, O, PACK], BF16, name="w2_grouped", align_bytes=64)
+        w2_codes = const.tile([P, O], U32, name="w2_codes", align_bytes=64)
+        w2_scales = const.tile([P, O], U8, name="w2_scales", align_bytes=64)
+        b1 = const.tile([P, PACK], BF16, name="b1")
+        b2 = const.tile([P, O], BF16, name="b2")
+        pick = const.tile([P, BG], F32, name="pick")
+
+        byte_tiles, wide, scaled, grouped, codes, scales, accs, turned = {}, {}, {}, {}, {}, {}, {}, {}
+        acc_sb, m1_codes, m1_scales, m1_ps, o_ps, o_pre = {}, {}, {}, {}, {}, {}
+
+        def load(g):
+            t = bytes_pool.tile([P, RUN * F], U8, name="x_in")
+            q, j = g // GPB, g % GPB
+            nc.sync.dma_start(out=t[:], in_=x_view[q, :, j * RUN * F : (j + 1) * RUN * F])
+            byte_tiles[g] = t
+
+        def widen(g):
+            for k in range(RUN):
+                t = wide_pool.tile([P, F], BF16, name="x_wide")
+                nc.scalar.copy(out=t[:], in_=byte_tiles[g][:, k * F : (k + 1) * F].bitcast(FP8))
+                wide[g, k] = t
+                if PATHS[g][k] == "E":
+                    s = scaled_pool.tile([P, F], BF16, name="x_scaled")
+                    nc.gpsimd.tensor_tensor(out=s[:], in0=t[:], in1=scale_nat[:], op=MULT)
+                    wide[g, k] = s
+
+        def turn(src, name):
+            bank = turn_psum.tile([P, 512], F32, name="bank")
+            words = src.bitcast(F32)
+            for u in range(2):
+                for c in range(PASSES):
+                    at = (u * PASSES + c) * P
+                    nc.tensor.transpose(bank[:, at : at + P], words[:, 256 * c + u : 256 * (c + 1) : 2], ident[:])
+            return bank
+
+        def evac(g, k):
+            pair = (g, k // 2)
+            if k % 2 == 0:
+                gt = grouped_pool.tile([P, 2 * F], BF16, name="x_grouped", align_bytes=64)
+                grouped[pair] = gt
+            half = grouped[pair][:, (k % 2) * F : (k % 2 + 1) * F]
+            bank = turned[g, k]
+            if PATHS[g][k] == "E":
+                nc.scalar.copy(
+                    out=half.bitcast(F32).rearrange("p (n u) -> p n u", u=2),
+                    in_=bank[:].rearrange("p (u n) -> p n u", u=2),
+                )
+            else:
+                nc.vector.tensor_tensor(
+                    out=half.rearrange("p (c r u e) -> p c r u e", c=PASSES, u=2, e=2),
+                    in0=bank[:].bitcast(BF16).rearrange("p (u c r e) -> p c r u e", u=2, c=PASSES, e=2),
+                    in1=scale_t[:]
+                    .rearrange("p c (u e) -> p c u e", u=2)
+                    .unsqueeze(2)
+                    .to_broadcast([P, PASSES, P, 2, 2]),
+                    op=MULT,
+                )
+
+        def quantize(g, h):
+            ct = code_pool.tile([P, 2 * PASSES * P], U32, name="x_codes", align_bytes=64)
+            st = code_pool.tile([P, 2 * PASSES * P], U8, name="x_scales", align_bytes=64)
+            nc.vector.quantize_mx(out=ct[:].bitcast(FP8X4), scales=st[:], in_=grouped[g, h][:])
+            codes[g, h], scales[g, h] = ct, st
+
+        def multiply(g):
+            q = g // GPB
+            if g % GPB == 0:
+                at = acc_psum.tile([P, G], F32, name="acc")
+                accs[q] = at
+            for k in range(RUN):
+                for c in range(PASSES):
+                    cols = slice(((k % 2) * PASSES + c) * P, ((k % 2) * PASSES + c + 1) * P)
+                    nc.tensor.matmul_mx(
+                        out=accs[q][:],
+                        lhsT=codes[g, k // 2][:, cols].bitcast(FP8X4),
+                        lhsT_scale=scales[g, k // 2][:, cols],
+                        rhs=w1_codes[:, c, :].bitcast(FP8X4),
+                        rhs_scale=w1_scales[:, c, :],
+                        start=(g % GPB == 0 and k == 0 and c == 0),
+                        stop=(g % GPB == GPB - 1 and k == RUN - 1 and c == PASSES - 1),
+                    )
+
+        nc.sync.dma_start(out=scale_t[:], in_=scale_row.rearrange("(c p t) -> p c t", c=PASSES, t=PACK))
+        load(0)
+        nc.sync.dma_start(out=w1[:], in_=W1g.rearrange("(p t) k -> p t k", t=PACK))
+        load(1)
+        nc.sync.dma_start(out=scale_nat[:], in_=scale_row.partition_broadcast(P))
+        nc.sync.dma_start(out=w2[:], in_=W2g)
+        nc.sync.dma_start(out=b1[:], in_=b1g.rearrange("(p t) -> p t", t=PACK))
+        nc.sync.dma_start(out=b2[:], in_=b2g.partition_broadcast(P))
+        load(2)
+        make_identity(nc, ident[:])
+        nc.vector.tensor_reduce(
+            out=pick[:], in_=ident[:].rearrange("p (b h) -> p b h", h=H), axis=mybir.AxisListType.X, op=ADD
+        )
+
+        with tc.manual_schedule():
+            widen(0)
+            widen(1)
+            for g in range(GROUPS + 3):
+                if g + 3 < GROUPS:
+                    load(g + 3)
+                qa = (g - 5) // GPB if g >= 5 and (g - 5) % GPB == 0 else None
+                qb = (g - 6) // GPB if g >= 6 and (g - 6) % GPB == 0 else None
+                if qa is not None:
+                    at = work.tile([P, G], F32, name="acc_copy")
+                    nc.scalar.copy(out=at[:], in_=accs[qa][:])
+                    acc_sb[qa] = at
+                if g < GROUPS:
+                    for k in range(RUN):
+                        turned[g, k] = turn(wide[g, k][:], "x")
+                    evac(g, 0)
+                    evac(g, 1)
+                if 1 <= g <= GROUPS:
+                    quantize(g - 1, 1)
+                if qa is not None:
+                    mp = small_psum.tile([P, 512], F32, name="small")
+                    for t in range(PACK):
+                        nc.tensor.matmul(
+                            mp[:, t * BG : (t + 1) * BG],
+                            lhsT=acc_sb[qa][:, t * P : (t + 1) * P],
+                            rhs=pick[:],
+                            start=True,
+                            stop=True,
+                        )
+                    m1_ps[qa] = mp
+                if qb is not None:
+                    op = small_psum.tile([P, 512], F32, name="small")
+                    nc.tensor.matmul_mx(
+                        out=op[:, :O],
+                        lhsT=m1_codes[qb][:].bitcast(FP8X4),
+                        lhsT_scale=m1_scales[qb][:],
+                        rhs=w2_codes[:].bitcast(FP8X4),
+                        rhs_scale=w2_scales[:],
+                        start=True,
+                        stop=True,
+                    )
+                    o_ps[qb] = op
+                if 1 <= g <= GROUPS:
+                    multiply(g - 1)
+                if g < GROUPS:
+                    evac(g, 2)
+                if qa is not None:
+                    pre = work.tile([P, BG, PACK], F32, name="m1_pre")
+                    nc.vector.scalar_tensor_tensor(
+                        out=pre[:],
+                        in0=m1_ps[qa][:, : PACK * BG].rearrange("p (t b) -> p b t", t=PACK),
+                        scalar=1.0 / NODES,
+                        in1=b1[:].unsqueeze(1).to_broadcast([P, BG, PACK]),
+                        op0=MULT,
+                        op1=ADD,
+                    )
+                if qb is not None:
+                    ot = work.tile([P, O], F32, name="o_pre")
+                    nc.vector.tensor_tensor(out=ot[:], in0=o_ps[qb][:, :O], in1=b2[:], op=ADD)
+                    o_pre[qb] = ot
+                if g < GROUPS:
+                    evac(g, 3)
+                if qa is not None:
+                    m1 = work.tile([P, BG, H, PACK], BF16, name="m1", align_bytes=64)
+                    nc.vector.tensor_scalar(
+                        out=m1[:],
+                        in0=pre[:].unsqueeze(2).to_broadcast([P, BG, H, PACK]),
+                        scalar1=0.0,
+                        scalar2=None,
+                        op0=MAX,
+                    )
+                if g < GROUPS:
+                    quantize(g, 0)
+                if qa is not None:
+                    mc = work.tile([P, P], U32, name="m1_codes", align_bytes=64)
+                    ms = work.tile([P, P], U8, name="m1_scales", align_bytes=64)
+                    nc.vector.quantize_mx(
+                        out=mc[:].bitcast(FP8X4), scales=ms[:], in_=m1[:].rearrange("p b h t -> p (b h t)")
+                    )
+                    m1_codes[qa], m1_scales[qa] = mc, ms
+                if qb is not None:
+                    rows = work.tile([P, REPS, O], F32, name="out_rows")
+                    nc.scalar.activation(
+                        out=rows[:], in_=o_pre[qb][:].unsqueeze(1).to_broadcast([P, REPS, O]), func=RELU
+                    )
+                    nc.sync.dma_start(
+                        out=out_view[qb].rearrange("p (a n) -> p a n", n=REPS * O),
+                        in_=rows[:]
+                        .rearrange("p r o -> p (r o)")
+                        .unsqueeze(1)
+                        .to_broadcast([P, SLOTS // REPS, REPS * O]),
+                    )
+                if g == 0:
+                    for t in range(PACK):
+                        bank = turn(w1[:, t, :], "w")
+                        for c in range(PASSES):
+                            dst = w1_grouped[:, c, t * P : (t + 1) * P, :].rearrange("p n t -> p (n t)").bitcast(F32)
+                            src = bank[:].rearrange("p (u c n) -> p c n u", u=2, c=PASSES)[:, c]
+                            dst = dst.rearrange("p (n u) -> p n u", u=2)
+                            if t % 2 == 0:
+                                nc.vector.tensor_copy(out=dst, in_=src)
+                            else:
+                                nc.scalar.copy(out=dst, in_=src)
+                    for c in range(PASSES):
+                        nc.vector.quantize_mx(
+                            out=w1_codes[:, c, :].bitcast(FP8X4),
+                            scales=w1_scales[:, c, :],
+                            in_=w1_grouped[:, c].rearrange("p n t -> p (n t)"),
+                        )
+                if g == 1:
+                    bank = turn_psum.tile([P, 512], F32, name="bank")
+                    words = w2[:].bitcast(F32)
+                    for u in range(2):
+                        nc.tensor.transpose(bank[:, u * P : (u + 1) * P], words[:, u:256:2], ident[:])
+                    nc.vector.tensor_copy(
+                        out=w2_grouped[:].rearrange("p n t -> p (n t)").bitcast(F32).rearrange("p (n u) -> p n u", u=2),
+                        in_=bank[:, : 2 * P].rearrange("p (u n) -> p n u", u=2),
+                    )
+                    nc.vector.quantize_mx(
+                        out=w2_codes[:].bitcast(FP8X4),
+                        scales=w2_scales[:],
+                        in_=w2_grouped[:].rearrange("p n t -> p (n t)"),
+                    )
+                if g + 2 < GROUPS:
+                    widen(g + 2)

@@ -28,7 +28,9 @@ RUN = 4
 GROUPS = BATCHES * SLOTS // RUN
 GPB = SLOTS // RUN
 REPS = 4
-PATHS = ["CCCC"] + ["ECCC"] * (GROUPS - 1)
+AHEAD = 2
+LOADS = 4
+PATHS = ["CCCC", "CCCC"] + ["CCCE"] * (GROUPS - 2)
 
 
 def tile_gcn_pa_t_kernel(tc, x_bytes, x_scale, W1g, b1g, W2g, b2g, out):
@@ -39,11 +41,11 @@ def tile_gcn_pa_t_kernel(tc, x_bytes, x_scale, W1g, b1g, W2g, b2g, out):
 
     with ExitStack() as ctx:
         const = ctx.enter_context(tc.tile_pool(name="const", bufs=1))
-        bytes_pool = ctx.enter_context(tc.tile_pool(name="bytes_pool", bufs=4))
-        wide_pool = ctx.enter_context(tc.tile_pool(name="wide_pool", bufs=12))
-        scaled_pool = ctx.enter_context(tc.tile_pool(name="scaled_pool", bufs=3))
-        grouped_pool = ctx.enter_context(tc.tile_pool(name="grouped_pool", bufs=4))
-        code_pool = ctx.enter_context(tc.tile_pool(name="code_pool", bufs=5))
+        bytes_pool = ctx.enter_context(tc.tile_pool(name="bytes_pool", bufs=LOADS + 1))
+        wide_pool = ctx.enter_context(tc.tile_pool(name="wide_pool", bufs=16))
+        scaled_pool = ctx.enter_context(tc.tile_pool(name="scaled_pool", bufs=16))
+        grouped_pool = ctx.enter_context(tc.tile_pool(name="grouped_pool", bufs=6))
+        code_pool = ctx.enter_context(tc.tile_pool(name="code_pool", bufs=6))
         work = ctx.enter_context(tc.tile_pool(name="work", bufs=2))
         turn_psum = ctx.enter_context(tc.psum_pool(name="turn_psum", bufs=5))
         acc_psum = ctx.enter_context(tc.psum_pool(name="acc_psum", bufs=2))
@@ -52,6 +54,7 @@ def tile_gcn_pa_t_kernel(tc, x_bytes, x_scale, W1g, b1g, W2g, b2g, out):
         ident = const.tile([P, P], F32, name="ident")
         scale_t = const.tile([P, PASSES, PACK], F32, name="scale_t")
         scale_nat = const.tile([P, F], F32, name="scale_nat")
+        scale_perm = const.tile([P, F], F32, name="scale_perm")
         w1 = const.tile([P, PACK, F], BF16, name="w1")
         w1_grouped = const.tile([P, PASSES, G, PACK], BF16, name="w1_grouped", align_bytes=64)
         w1_codes = const.tile([P, PASSES, G], U32, name="w1_codes", align_bytes=64)
@@ -64,50 +67,92 @@ def tile_gcn_pa_t_kernel(tc, x_bytes, x_scale, W1g, b1g, W2g, b2g, out):
         b2 = const.tile([P, O], BF16, name="b2")
         pick = const.tile([P, BG], F32, name="pick")
 
-        byte_tiles, wide, scaled, grouped, codes, scales, accs, turned = {}, {}, {}, {}, {}, {}, {}, {}
-        acc_sb, m1_codes, m1_scales, m1_ps, o_ps, o_pre = {}, {}, {}, {}, {}, {}
+        byte_tiles, wide, grouped, codes, scales, accs, turned = {}, {}, {}, {}, {}, {}, {}
+        acc_sb, m1_codes, m1_scales, m1_ps, m1_pre, o_ps, o_pre = {}, {}, {}, {}, {}, {}, {}
 
-        def load(g):
+        def load(g, split=1):
             t = bytes_pool.tile([P, RUN * F], U8, name="x_in")
             q, j = g // GPB, g % GPB
-            nc.sync.dma_start(out=t[:], in_=x_view[q, :, j * RUN * F : (j + 1) * RUN * F])
+            n = RUN * F // split
+            for i in range(split):
+                nc.sync.dma_start(
+                    out=t[:, i * n : (i + 1) * n], in_=x_view[q, :, j * RUN * F + i * n : j * RUN * F + (i + 1) * n]
+                )
             byte_tiles[g] = t
 
         def widen(g):
-            for k in range(RUN):
+            order = sorted(range(RUN), key=lambda k: "EPCA".index(PATHS[g][k]))
+            for k in order:
+                src = byte_tiles[g][:, k * F : (k + 1) * F].bitcast(FP8)
+                if PATHS[g][k] == "A":
+                    continue
                 t = wide_pool.tile([P, F], BF16, name="x_wide")
-                nc.scalar.copy(out=t[:], in_=byte_tiles[g][:, k * F : (k + 1) * F].bitcast(FP8))
+                nc.scalar.copy(out=t[:], in_=src)
                 wide[g, k] = t
+                if PATHS[g][k] == "P":
+                    s = scaled_pool.tile([P, F], BF16, name="x_scaled")
+                    nc.scalar.copy(
+                        out=s[:].bitcast(F32).rearrange("p (u n) -> p u n", u=2),
+                        in_=t[:].bitcast(F32).rearrange("p (n u) -> p u n", u=2),
+                    )
+                    wide[g, k] = s
                 if PATHS[g][k] == "E":
                     s = scaled_pool.tile([P, F], BF16, name="x_scaled")
-                    nc.gpsimd.tensor_tensor(out=s[:], in0=t[:], in1=scale_nat[:], op=MULT)
+                    nc.vector.memset(s[:, 0:2], 0.0)
+                    for i in range(4):
+                        part = slice(i * F // 4, (i + 1) * F // 4)
+                        words = slice(i % 2 * 256 // 2, (i % 2 + 1) * 256 // 2)
+                        nc.gpsimd.tensor_tensor(
+                            out=s[:, part].rearrange("p (n e) -> p n e", e=2),
+                            in0=t[:].rearrange("p (n u e) -> p u n e", u=2, e=2)[:, i // 2, words],
+                            in1=scale_perm[:, part].rearrange("p (n e) -> p n e", e=2),
+                            op=MULT,
+                        )
                     wide[g, k] = s
 
-        def turn(src, name):
+        def widen_v(g):
+            for k in range(RUN):
+                if PATHS[g][k] == "A":
+                    s = scaled_pool.tile([P, F], BF16, name="x_scaled")
+                    nc.vector.tensor_tensor(
+                        out=s[:], in0=byte_tiles[g][:, k * F : (k + 1) * F].bitcast(FP8), in1=scale_nat[:], op=MULT
+                    )
+                    wide[g, k] = s
+
+        def turn(src, perm=False):
             bank = turn_psum.tile([P, 512], F32, name="bank")
             words = src.bitcast(F32)
             for u in range(2):
                 for c in range(PASSES):
                     at = (u * PASSES + c) * P
-                    nc.tensor.transpose(bank[:, at : at + P], words[:, 256 * c + u : 256 * (c + 1) : 2], ident[:])
+                    cols = slice(at, at + P) if perm else slice(256 * c + u, 256 * (c + 1), 2)
+                    nc.tensor.transpose(bank[:, at : at + P], words[:, cols], ident[:])
             return bank
 
-        def evac(g, k):
+        def turn_group(g):
+            for k in sorted(range(RUN), key=lambda k: "EACP".index(PATHS[g][k])):
+                turned[g, k] = turn(wide[g, k][:], PATHS[g][k] in "EP")
+
+        def half(g, k):
             pair = (g, k // 2)
-            if k % 2 == 0:
+            if pair not in grouped:
                 gt = grouped_pool.tile([P, 2 * F], BF16, name="x_grouped", align_bytes=64)
                 grouped[pair] = gt
-            half = grouped[pair][:, (k % 2) * F : (k % 2 + 1) * F]
-            bank = turned[g, k]
-            if PATHS[g][k] == "E":
-                nc.scalar.copy(
-                    out=half.bitcast(F32).rearrange("p (n u) -> p n u", u=2),
-                    in_=bank[:].rearrange("p (u n) -> p n u", u=2),
-                )
-            else:
+            return grouped[pair][:, (k % 2) * F : (k % 2 + 1) * F]
+
+        def evac_s(g):
+            for k in range(RUN):
+                if PATHS[g][k] in "EA":
+                    nc.scalar.copy(
+                        out=half(g, k).bitcast(F32).rearrange("p (n u) -> p n u", u=2),
+                        in_=turned[g, k][:].rearrange("p (u n) -> p n u", u=2),
+                    )
+
+        def evac_v(g, k):
+            if PATHS[g][k] in "CP":
                 nc.vector.tensor_tensor(
-                    out=half.rearrange("p (c r u e) -> p c r u e", c=PASSES, u=2, e=2),
-                    in0=bank[:].bitcast(BF16).rearrange("p (u c r e) -> p c r u e", u=2, c=PASSES, e=2),
+                    out=half(g, k).rearrange("p (c r u e) -> p c r u e", c=PASSES, u=2, e=2),
+                    in0=turned[g, k][:].bitcast(BF16).rearrange("p (u c r e) -> p c r u e", u=2, c=PASSES, e=2),
                     in1=scale_t[:]
                     .rearrange("p c (u e) -> p c u e", u=2)
                     .unsqueeze(2)
@@ -140,38 +185,33 @@ def tile_gcn_pa_t_kernel(tc, x_bytes, x_scale, W1g, b1g, W2g, b2g, out):
                     )
 
         nc.sync.dma_start(out=scale_t[:], in_=scale_row.rearrange("(c p t) -> p c t", c=PASSES, t=PACK))
-        load(0)
+        load(0, 4)
         nc.sync.dma_start(out=w1[:], in_=W1g.rearrange("(p t) k -> p t k", t=PACK))
         load(1)
         nc.sync.dma_start(out=scale_nat[:], in_=scale_row.partition_broadcast(P))
         nc.sync.dma_start(out=w2[:], in_=W2g)
         nc.sync.dma_start(out=b1[:], in_=b1g.rearrange("(p t) -> p t", t=PACK))
         nc.sync.dma_start(out=b2[:], in_=b2g.partition_broadcast(P))
-        load(2)
+        for g in range(2, LOADS):
+            load(g)
         make_identity(nc, ident[:])
         nc.vector.tensor_reduce(
             out=pick[:], in_=ident[:].rearrange("p (b h) -> p b h", h=H), axis=mybir.AxisListType.X, op=ADD
         )
 
         with tc.manual_schedule():
-            widen(0)
-            widen(1)
+            for g in range(AHEAD):
+                widen(g)
+                widen_v(g)
             for g in range(GROUPS + 3):
-                if g + 3 < GROUPS:
-                    load(g + 3)
-                qa = (g - 5) // GPB if g >= 5 and (g - 5) % GPB == 0 else None
-                qb = (g - 6) // GPB if g >= 6 and (g - 6) % GPB == 0 else None
-                if qa is not None:
-                    at = work.tile([P, G], F32, name="acc_copy")
-                    nc.scalar.copy(out=at[:], in_=accs[qa][:])
-                    acc_sb[qa] = at
+                if g + LOADS < GROUPS:
+                    load(g + LOADS)
+                qa = (g - 1) // GPB - 1 if g > GPB and g % GPB == 1 else None
+                qb = (g - 2) // GPB - 1 if g > GPB and g % GPB == 2 else None
                 if g < GROUPS:
-                    for k in range(RUN):
-                        turned[g, k] = turn(wide[g, k][:], "x")
-                    evac(g, 0)
-                    evac(g, 1)
-                if 1 <= g <= GROUPS:
-                    quantize(g - 1, 1)
+                    turn_group(g)
+                    evac_s(g)
+                    evac_v(g, 0)
                 if qa is not None:
                     mp = small_psum.tile([P, 512], F32, name="small")
                     for t in range(PACK):
@@ -195,10 +235,21 @@ def tile_gcn_pa_t_kernel(tc, x_bytes, x_scale, W1g, b1g, W2g, b2g, out):
                         stop=True,
                     )
                     o_ps[qb] = op
+                if g == 0:
+                    for t in range(PACK):
+                        bank = turn(w1[:, t, :])
+                        for c in range(PASSES):
+                            dst = w1_grouped[:, c, t * P : (t + 1) * P, :].rearrange("p n t -> p (n t)").bitcast(F32)
+                            src = bank[:].rearrange("p (u c n) -> p c n u", u=2, c=PASSES)[:, c]
+                            dst = dst.rearrange("p (n u) -> p n u", u=2)
+                            nc.scalar.copy(out=dst, in_=src)
                 if 1 <= g <= GROUPS:
                     multiply(g - 1)
                 if g < GROUPS:
-                    evac(g, 2)
+                    evac_v(g, 1)
+                    if g == GROUPS - 1:
+                        quantize(g, 0)
+                    evac_v(g, 2)
                 if qa is not None:
                     pre = work.tile([P, BG, PACK], F32, name="m1_pre")
                     nc.vector.scalar_tensor_tensor(
@@ -214,7 +265,10 @@ def tile_gcn_pa_t_kernel(tc, x_bytes, x_scale, W1g, b1g, W2g, b2g, out):
                     nc.vector.tensor_tensor(out=ot[:], in0=o_ps[qb][:, :O], in1=b2[:], op=ADD)
                     o_pre[qb] = ot
                 if g < GROUPS:
-                    evac(g, 3)
+                    evac_v(g, 3)
+                    qs = [0, 1] if PATHS[g][3] in "EA" or PATHS[g][2] in "CP" else [1, 0]
+                    if g < GROUPS - 1:
+                        quantize(g, qs[0])
                 if qa is not None:
                     m1 = work.tile([P, BG, H, PACK], BF16, name="m1", align_bytes=64)
                     nc.vector.tensor_scalar(
@@ -224,8 +278,20 @@ def tile_gcn_pa_t_kernel(tc, x_bytes, x_scale, W1g, b1g, W2g, b2g, out):
                         scalar2=None,
                         op0=MAX,
                     )
+                if g == 0:
+                    for c in range(PASSES):
+                        nc.vector.quantize_mx(
+                            out=w1_codes[:, c, :].bitcast(FP8X4),
+                            scales=w1_scales[:, c, :],
+                            in_=w1_grouped[:, c].rearrange("p n t -> p (n t)"),
+                        )
                 if g < GROUPS:
-                    quantize(g, 0)
+                    quantize(g, qs[1])
+                if g == 0:
+                    nc.vector.tensor_copy(
+                        out=scale_perm[:].rearrange("p (u n e) -> p u n e", u=2, e=2),
+                        in_=scale_nat[:].rearrange("p (n u e) -> p u n e", u=2, e=2),
+                    )
                 if qa is not None:
                     mc = work.tile([P, P], U32, name="m1_codes", align_bytes=64)
                     ms = work.tile([P, P], U8, name="m1_scales", align_bytes=64)
@@ -245,23 +311,6 @@ def tile_gcn_pa_t_kernel(tc, x_bytes, x_scale, W1g, b1g, W2g, b2g, out):
                         .unsqueeze(1)
                         .to_broadcast([P, SLOTS // REPS, REPS * O]),
                     )
-                if g == 0:
-                    for t in range(PACK):
-                        bank = turn(w1[:, t, :], "w")
-                        for c in range(PASSES):
-                            dst = w1_grouped[:, c, t * P : (t + 1) * P, :].rearrange("p n t -> p (n t)").bitcast(F32)
-                            src = bank[:].rearrange("p (u c n) -> p c n u", u=2, c=PASSES)[:, c]
-                            dst = dst.rearrange("p (n u) -> p n u", u=2)
-                            if t % 2 == 0:
-                                nc.vector.tensor_copy(out=dst, in_=src)
-                            else:
-                                nc.scalar.copy(out=dst, in_=src)
-                    for c in range(PASSES):
-                        nc.vector.quantize_mx(
-                            out=w1_codes[:, c, :].bitcast(FP8X4),
-                            scales=w1_scales[:, c, :],
-                            in_=w1_grouped[:, c].rearrange("p n t -> p (n t)"),
-                        )
                 if g == 1:
                     bank = turn_psum.tile([P, 512], F32, name="bank")
                     words = w2[:].bitcast(F32)
@@ -276,5 +325,13 @@ def tile_gcn_pa_t_kernel(tc, x_bytes, x_scale, W1g, b1g, W2g, b2g, out):
                         scales=w2_scales[:],
                         in_=w2_grouped[:].rearrange("p n t -> p (n t)"),
                     )
-                if g + 2 < GROUPS:
-                    widen(g + 2)
+                if g + AHEAD < GROUPS:
+                    widen(g + AHEAD)
+                    widen_v(g + AHEAD)
+                if g >= GPB and g % GPB == 0:
+                    q = g // GPB - 1
+                    at = work.tile([P, G], F32, name="acc_copy")
+                    for i in range(2):
+                        part = slice(i * G // 2, (i + 1) * G // 2)
+                        nc.scalar.copy(out=at[:, part], in_=accs[q][:, part])
+                    acc_sb[q] = at

@@ -24,13 +24,14 @@ BATCHES = 4
 BG = GRAPHS // BATCHES
 H = P // BG
 SLOTS = NODES // H
-RUN = 4
-GROUPS = BATCHES * SLOTS // RUN
-GPB = SLOTS // RUN
+CHUNK = 4
+LOADS = 7
 REPS = 4
-AHEAD = 2
-LOADS = 4
-PATHS = ["CCCC", "CCCC"] + ["CCCE"] * (GROUPS - 2)
+
+RUNS = ["CCCC", "CCCC"] + ["CCCE", "CCAE"] * 7
+FIRST = [sum(len(run) for run in RUNS[:r]) for r in range(len(RUNS))]
+KIND = "".join(RUNS)
+LOOK = 8
 
 
 def tile_gcn_pa_t_kernel(tc, x_bytes, x_scale, W1g, b1g, W2g, b2g, out):
@@ -38,6 +39,7 @@ def tile_gcn_pa_t_kernel(tc, x_bytes, x_scale, W1g, b1g, W2g, b2g, out):
     x_view = x_bytes.rearrange("(q b) (h c) d f -> q (b h) (c d f)", q=BATCHES, h=H)
     out_view = out.rearrange("(q b) (h s) o -> q (b h) (s o)", q=BATCHES, h=H)
     scale_row = x_scale.rearrange("a b c f -> (a b c f)")
+    w1_view = W1g.rearrange("(p t) k -> p t k", t=PACK)
 
     with ExitStack() as ctx:
         const = ctx.enter_context(tc.tile_pool(name="const", bufs=1))
@@ -45,7 +47,7 @@ def tile_gcn_pa_t_kernel(tc, x_bytes, x_scale, W1g, b1g, W2g, b2g, out):
         wide_pool = ctx.enter_context(tc.tile_pool(name="wide_pool", bufs=16))
         scaled_pool = ctx.enter_context(tc.tile_pool(name="scaled_pool", bufs=16))
         grouped_pool = ctx.enter_context(tc.tile_pool(name="grouped_pool", bufs=6))
-        code_pool = ctx.enter_context(tc.tile_pool(name="code_pool", bufs=6))
+        code_pool = ctx.enter_context(tc.tile_pool(name="code_pool", bufs=8))
         work = ctx.enter_context(tc.tile_pool(name="work", bufs=2))
         turn_psum = ctx.enter_context(tc.psum_pool(name="turn_psum", bufs=5))
         acc_psum = ctx.enter_context(tc.psum_pool(name="acc_psum", bufs=2))
@@ -60,250 +62,298 @@ def tile_gcn_pa_t_kernel(tc, x_bytes, x_scale, W1g, b1g, W2g, b2g, out):
         w1_codes = const.tile([P, PASSES, G], U32, name="w1_codes", align_bytes=64)
         w1_scales = const.tile([P, PASSES, G], U8, name="w1_scales", align_bytes=64)
         w2 = const.tile([P, G], BF16, name="w2")
-        w2_grouped = const.tile([P, O, PACK], BF16, name="w2_grouped", align_bytes=64)
+        w2_grouped = const.tile([P, O * PACK], BF16, name="w2_grouped", align_bytes=64)
         w2_codes = const.tile([P, O], U32, name="w2_codes", align_bytes=64)
         w2_scales = const.tile([P, O], U8, name="w2_scales", align_bytes=64)
         b1 = const.tile([P, PACK], BF16, name="b1")
         b2 = const.tile([P, O], BF16, name="b2")
         pick = const.tile([P, BG], F32, name="pick")
 
-        byte_tiles, wide, grouped, codes, scales, accs, turned = {}, {}, {}, {}, {}, {}, {}
-        acc_sb, m1_codes, m1_scales, m1_ps, m1_pre, o_ps, o_pre = {}, {}, {}, {}, {}, {}, {}
+        chunks, ready, tokened, turned, grouped, codes, scales = {}, {}, {}, {}, {}, {}, {}
+        accs, acc_sb, m1_ps, m1_pre, o_ps, o_pre = {}, {}, {}, {}, {}, {}
 
-        def load(g, split=1):
-            t = bytes_pool.tile([P, RUN * F], U8, name="x_in")
-            q, j = g // GPB, g % GPB
-            n = RUN * F // split
+        def load(chunk, split=1):
+            t = bytes_pool.tile([P, CHUNK * F], U8, name="x_in")
+            q, at = divmod(chunk * CHUNK, SLOTS)
+            n = CHUNK * F // split
             for i in range(split):
                 nc.sync.dma_start(
-                    out=t[:, i * n : (i + 1) * n], in_=x_view[q, :, j * RUN * F + i * n : j * RUN * F + (i + 1) * n]
+                    out=t[:, i * n : (i + 1) * n], in_=x_view[q, :, at * F + i * n : at * F + (i + 1) * n]
                 )
-            byte_tiles[g] = t
+            chunks[chunk] = t
 
-        def widen(g):
-            order = sorted(range(RUN), key=lambda k: "EPCA".index(PATHS[g][k]))
-            for k in order:
-                src = byte_tiles[g][:, k * F : (k + 1) * F].bitcast(FP8)
-                if PATHS[g][k] == "A":
-                    continue
-                t = wide_pool.tile([P, F], BF16, name="x_wide")
-                nc.scalar.copy(out=t[:], in_=src)
-                wide[g, k] = t
-                if PATHS[g][k] == "P":
-                    s = scaled_pool.tile([P, F], BF16, name="x_scaled")
+        def slot_bytes(s):
+            return chunks[s // CHUNK][:, s % CHUNK * F : (s % CHUNK + 1) * F].bitcast(FP8)
+
+        def slots_of(r, kinds):
+            return [s for s in range(FIRST[r], FIRST[r] + len(RUNS[r])) if KIND[s] in kinds]
+
+        def token(r):
+            for s in slots_of(r, "E"):
+                t = scaled_pool.tile([P, F], BF16, name="x_scaled")
+                nc.vector.memset(t[:, 0:2], 0.0)
+                tokened[s] = t
+
+        def scale_on_vector(r):
+            for s in slots_of(r, "A"):
+                t = scaled_pool.tile([P, F], BF16, name="x_scaled")
+                nc.vector.tensor_tensor(out=t[:], in0=slot_bytes(s), in1=scale_nat[:], op=MULT)
+                ready[s] = t
+
+        def widen(r):
+            for s in slots_of(r, "E") + slots_of(r, "PC"):
+                wide = wide_pool.tile([P, F], BF16, name="x_wide")
+                nc.scalar.copy(out=wide[:], in_=slot_bytes(s))
+                ready[s] = wide
+                if KIND[s] == "P":
+                    t = scaled_pool.tile([P, F], BF16, name="x_scaled")
                     nc.scalar.copy(
-                        out=s[:].bitcast(F32).rearrange("p (u n) -> p u n", u=2),
-                        in_=t[:].bitcast(F32).rearrange("p (n u) -> p u n", u=2),
+                        out=t[:].bitcast(F32).rearrange("p (u n) -> p u n", u=2),
+                        in_=wide[:].bitcast(F32).rearrange("p (n u) -> p u n", u=2),
                     )
-                    wide[g, k] = s
-                if PATHS[g][k] == "E":
-                    s = scaled_pool.tile([P, F], BF16, name="x_scaled")
-                    nc.vector.memset(s[:, 0:2], 0.0)
-                    for i in range(4):
-                        part = slice(i * F // 4, (i + 1) * F // 4)
-                        words = slice(i % 2 * 256 // 2, (i % 2 + 1) * 256 // 2)
+                    ready[s] = t
+                if KIND[s] == "E":
+                    t = tokened[s]
+                    for u in range(2):
+                        half = slice(u * F // 2, (u + 1) * F // 2)
                         nc.gpsimd.tensor_tensor(
-                            out=s[:, part].rearrange("p (n e) -> p n e", e=2),
-                            in0=t[:].rearrange("p (n u e) -> p u n e", u=2, e=2)[:, i // 2, words],
-                            in1=scale_perm[:, part].rearrange("p (n e) -> p n e", e=2),
+                            out=t[:, half].rearrange("p (n e) -> p n e", e=2),
+                            in0=wide[:].rearrange("p (n u e) -> p u n e", u=2, e=2)[:, u],
+                            in1=scale_perm[:, half].rearrange("p (n e) -> p n e", e=2),
                             op=MULT,
                         )
-                    wide[g, k] = s
+                    ready[s] = t
 
-        def widen_v(g):
-            for k in range(RUN):
-                if PATHS[g][k] == "A":
-                    s = scaled_pool.tile([P, F], BF16, name="x_scaled")
-                    nc.vector.tensor_tensor(
-                        out=s[:], in0=byte_tiles[g][:, k * F : (k + 1) * F].bitcast(FP8), in1=scale_nat[:], op=MULT
-                    )
-                    wide[g, k] = s
-
-        def turn(src, perm=False):
+        def turn(rows, in_order):
             bank = turn_psum.tile([P, 512], F32, name="bank")
-            words = src.bitcast(F32)
+            words = rows.bitcast(F32)
             for u in range(2):
                 for c in range(PASSES):
                     at = (u * PASSES + c) * P
-                    cols = slice(at, at + P) if perm else slice(256 * c + u, 256 * (c + 1), 2)
+                    cols = slice(at, at + P) if in_order else slice(256 * c + u, 256 * (c + 1), 2)
                     nc.tensor.transpose(bank[:, at : at + P], words[:, cols], ident[:])
             return bank
 
-        def turn_group(g):
-            for k in sorted(range(RUN), key=lambda k: "EACP".index(PATHS[g][k])):
-                turned[g, k] = turn(wide[g, k][:], PATHS[g][k] in "EP")
-
-        def half(g, k):
-            pair = (g, k // 2)
+        def half_of(s):
+            pair = s // 2
             if pair not in grouped:
-                gt = grouped_pool.tile([P, 2 * F], BF16, name="x_grouped", align_bytes=64)
-                grouped[pair] = gt
-            return grouped[pair][:, (k % 2) * F : (k % 2 + 1) * F]
+                t = grouped_pool.tile([P, 2 * F], BF16, name="x_grouped", align_bytes=64)
+                grouped[pair] = t
+            return grouped[pair][:, s % 2 * F : (s % 2 + 1) * F]
 
-        def evac_s(g):
-            for k in range(RUN):
-                if PATHS[g][k] in "EA":
-                    nc.scalar.copy(
-                        out=half(g, k).bitcast(F32).rearrange("p (n u) -> p n u", u=2),
-                        in_=turned[g, k][:].rearrange("p (u n) -> p n u", u=2),
-                    )
-
-        def evac_v(g, k):
-            if PATHS[g][k] in "CP":
-                nc.vector.tensor_tensor(
-                    out=half(g, k).rearrange("p (c r u e) -> p c r u e", c=PASSES, u=2, e=2),
-                    in0=turned[g, k][:].bitcast(BF16).rearrange("p (u c r e) -> p c r u e", u=2, c=PASSES, e=2),
-                    in1=scale_t[:]
-                    .rearrange("p c (u e) -> p c u e", u=2)
-                    .unsqueeze(2)
-                    .to_broadcast([P, PASSES, P, 2, 2]),
-                    op=MULT,
+        def empty_on_scalar(r):
+            for s in slots_of(r, "AE"):
+                nc.scalar.copy(
+                    out=half_of(s).bitcast(F32).rearrange("p (n u) -> p n u", u=2),
+                    in_=turned[s][:].rearrange("p (u n) -> p n u", u=2),
                 )
 
-        def quantize(g, h):
+        def empty_and_scale(s):
+            nc.vector.tensor_tensor(
+                out=half_of(s).rearrange("p (c r u e) -> p c r u e", c=PASSES, u=2, e=2),
+                in0=turned[s][:].bitcast(BF16).rearrange("p (u c r e) -> p c r u e", u=2, c=PASSES, e=2),
+                in1=scale_t[:]
+                .rearrange("p c (u e) -> p c u e", u=2)
+                .unsqueeze(2)
+                .to_broadcast([P, PASSES, P, 2, 2]),
+                op=MULT,
+            )
+
+        def quantize(pair):
             ct = code_pool.tile([P, 2 * PASSES * P], U32, name="x_codes", align_bytes=64)
             st = code_pool.tile([P, 2 * PASSES * P], U8, name="x_scales", align_bytes=64)
-            nc.vector.quantize_mx(out=ct[:].bitcast(FP8X4), scales=st[:], in_=grouped[g, h][:])
-            codes[g, h], scales[g, h] = ct, st
+            nc.vector.quantize_mx(out=ct[:].bitcast(FP8X4), scales=st[:], in_=grouped[pair][:])
+            codes[pair], scales[pair] = ct, st
 
-        def multiply(g):
-            q = g // GPB
-            if g % GPB == 0:
-                at = acc_psum.tile([P, G], F32, name="acc")
-                accs[q] = at
-            for k in range(RUN):
-                for c in range(PASSES):
-                    cols = slice(((k % 2) * PASSES + c) * P, ((k % 2) * PASSES + c + 1) * P)
+        def pairs_of(r):
+            pairs = [s // 2 for s in slots_of(r, "ACEP") if s % 2 == 0]
+            return pairs
+
+        def multiply(r):
+            q = FIRST[r] // SLOTS
+            if FIRST[r] % SLOTS == 0:
+                t = acc_psum.tile([P, G], F32, name="acc")
+                accs[q] = t
+            for pair in ORDER[r]:
+                for i in range(2 * PASSES):
+                    cols = slice(i * P, (i + 1) * P)
                     nc.tensor.matmul_mx(
                         out=accs[q][:],
-                        lhsT=codes[g, k // 2][:, cols].bitcast(FP8X4),
-                        lhsT_scale=scales[g, k // 2][:, cols],
-                        rhs=w1_codes[:, c, :].bitcast(FP8X4),
-                        rhs_scale=w1_scales[:, c, :],
-                        start=(g % GPB == 0 and k == 0 and c == 0),
-                        stop=(g % GPB == GPB - 1 and k == RUN - 1 and c == PASSES - 1),
+                        lhsT=codes[pair][:, cols].bitcast(FP8X4),
+                        lhsT_scale=scales[pair][:, cols],
+                        rhs=w1_codes[:, i % PASSES, :].bitcast(FP8X4),
+                        rhs_scale=w1_scales[:, i % PASSES, :],
+                        start=(FIRST[r] % SLOTS == 0 and pair == ORDER[r][0] and i == 0),
+                        stop=((FIRST[r] + len(RUNS[r])) % SLOTS == 0 and pair == ORDER[r][-1] and i == 2 * PASSES - 1),
                     )
 
+        def prepare_w1(t):
+            bank = turn(w1[:, t, :], False)
+            nc.vector.tensor_copy(
+                out=w1_grouped[:, :, t * P : (t + 1) * P, :]
+                .rearrange("p c n t -> p c (n t)")
+                .bitcast(F32)
+                .rearrange("p c (n u) -> p c n u", u=2),
+                in_=bank[:].rearrange("p (u c n) -> p c n u", u=2, c=PASSES),
+            )
+
+        for t in range(2):
+            nc.sync.dma_start(out=w1[:, t, :], in_=w1_view[:, t, :])
+        load(0, 2)
+        for t in range(2, 4):
+            nc.sync.dma_start(out=w1[:, t, :], in_=w1_view[:, t, :])
         nc.sync.dma_start(out=scale_t[:], in_=scale_row.rearrange("(c p t) -> p c t", c=PASSES, t=PACK))
-        load(0, 4)
-        nc.sync.dma_start(out=w1[:], in_=W1g.rearrange("(p t) k -> p t k", t=PACK))
         load(1)
         nc.sync.dma_start(out=scale_nat[:], in_=scale_row.partition_broadcast(P))
         nc.sync.dma_start(out=w2[:], in_=W2g)
         nc.sync.dma_start(out=b1[:], in_=b1g.rearrange("(p t) -> p t", t=PACK))
         nc.sync.dma_start(out=b2[:], in_=b2g.partition_broadcast(P))
-        for g in range(2, LOADS):
-            load(g)
+        for chunk in range(2, LOADS):
+            load(chunk)
         make_identity(nc, ident[:])
         nc.vector.tensor_reduce(
             out=pick[:], in_=ident[:].rearrange("p (b h) -> p b h", h=H), axis=mybir.AxisListType.X, op=ADD
         )
+        nc.gpsimd.tensor_copy(
+            out=scale_perm[:].rearrange("p (u n e) -> p u n e", u=2, e=2),
+            in_=scale_nat[:].rearrange("p (n u e) -> p u n e", u=2, e=2),
+        )
+
+        last_run = len(RUNS) - 1
+        ORDER = {}
+        for r in range(len(RUNS)):
+            vec = [p for p in pairs_of(r) if KIND[2 * p] in "CP" or KIND[2 * p + 1] in "CP"]
+            sca = [p for p in pairs_of(r) if p not in vec]
+            ORDER[r] = sca + vec if r >= last_run - 1 else vec + sca
+        ends = [r for r in range(len(RUNS)) if (FIRST[r] + len(RUNS[r])) % SLOTS == 0]
 
         with tc.manual_schedule():
-            for g in range(AHEAD):
-                widen(g)
-                widen_v(g)
-            for g in range(GROUPS + 3):
-                if g + LOADS < GROUPS:
-                    load(g + LOADS)
-                qa = (g - 1) // GPB - 1 if g > GPB and g % GPB == 1 else None
-                qb = (g - 2) // GPB - 1 if g > GPB and g % GPB == 2 else None
-                if g < GROUPS:
-                    turn_group(g)
-                    evac_s(g)
-                    evac_v(g, 0)
-                if qa is not None:
-                    mp = small_psum.tile([P, 512], F32, name="small")
+            prepared = 0
+            loaded = LOADS
+
+            for r in range(len(RUNS) + 3):
+                live = r < len(RUNS)
+                qm = ends.index(r - 1) if r - 1 in ends else None
+                qa = ends.index(r - 2) if r - 2 in ends else None
+                qb = ends.index(r - 3) if r - 3 in ends else None
+                end = FIRST[r] + len(RUNS[r]) if live else len(KIND)
+                upcoming = [n for n in range(prepared, len(RUNS)) if FIRST[n] < end + LOOK]
+                if r == 0:
+                    for n in upcoming[:2]:
+                        token(n)
+                        scale_on_vector(n)
+                        widen(n)
+                    prepared = 2
+                    upcoming = upcoming[2:]
                     for t in range(PACK):
+                        prepare_w1(t)
+                if loaded * CHUNK < len(KIND) and loaded * CHUNK < end + LOADS * CHUNK:
+                    load(loaded)
+                    loaded += 1
+                vec = slots_of(r, "CP") if live else []
+                if live:
+                    for s in slots_of(r, "A") + slots_of(r, "CP") + slots_of(r, "E"):
+                        bank = turn(ready[s][:], KIND[s] in "EP")
+                        turned[s] = bank
+                    empty_on_scalar(r)
+                for s in vec[:1]:
+                    empty_and_scale(s)
+                if qb is not None:
+                    m1 = work.tile([P, BG, H, PACK], BF16, name="m1", align_bytes=64)
+                    spread = m1_pre[qb][:].unsqueeze(2).to_broadcast([P, BG, H, PACK])
+                    nc.vector.tensor_scalar(out=m1[:], in0=spread, scalar1=0.0, scalar2=None, op0=MAX)
+                if 1 <= r <= len(RUNS):
+                    multiply(r - 1)
+                if qa is not None:
+                    t = small_psum.tile([P, 512], F32, name="small")
+                    for i in range(PACK):
                         nc.tensor.matmul(
-                            mp[:, t * BG : (t + 1) * BG],
-                            lhsT=acc_sb[qa][:, t * P : (t + 1) * P],
+                            t[:, i * BG : (i + 1) * BG],
+                            lhsT=acc_sb[qa][:, i * P : (i + 1) * P],
                             rhs=pick[:],
                             start=True,
                             stop=True,
                         )
-                    m1_ps[qa] = mp
+                    m1_ps[qa] = t
+                for s in vec[1:2]:
+                    empty_and_scale(s)
                 if qb is not None:
-                    op = small_psum.tile([P, 512], F32, name="small")
+                    mc = work.tile([P, P], U32, name="m1_codes", align_bytes=64)
+                    ms = work.tile([P, P], U8, name="m1_scales", align_bytes=64)
+                    nc.vector.quantize_mx(
+                        out=mc[:].bitcast(FP8X4), scales=ms[:], in_=m1[:].rearrange("p b h t -> p (b h t)")
+                    )
+                    t = small_psum.tile([P, 512], F32, name="small")
                     nc.tensor.matmul_mx(
-                        out=op[:, :O],
-                        lhsT=m1_codes[qb][:].bitcast(FP8X4),
-                        lhsT_scale=m1_scales[qb][:],
+                        out=t[:, :O],
+                        lhsT=mc[:].bitcast(FP8X4),
+                        lhsT_scale=ms[:],
                         rhs=w2_codes[:].bitcast(FP8X4),
                         rhs_scale=w2_scales[:],
                         start=True,
                         stop=True,
                     )
-                    o_ps[qb] = op
-                if g == 0:
-                    for t in range(PACK):
-                        bank = turn(w1[:, t, :])
-                        for c in range(PASSES):
-                            dst = w1_grouped[:, c, t * P : (t + 1) * P, :].rearrange("p n t -> p (n t)").bitcast(F32)
-                            src = bank[:].rearrange("p (u c n) -> p c n u", u=2, c=PASSES)[:, c]
-                            dst = dst.rearrange("p (n u) -> p n u", u=2)
-                            nc.scalar.copy(out=dst, in_=src)
-                if 1 <= g <= GROUPS:
-                    multiply(g - 1)
-                if g < GROUPS:
-                    evac_v(g, 1)
-                    if g == GROUPS - 1:
-                        quantize(g, 0)
-                    evac_v(g, 2)
-                if qa is not None:
-                    pre = work.tile([P, BG, PACK], F32, name="m1_pre")
-                    nc.vector.scalar_tensor_tensor(
-                        out=pre[:],
-                        in0=m1_ps[qa][:, : PACK * BG].rearrange("p (t b) -> p b t", t=PACK),
-                        scalar=1.0 / NODES,
-                        in1=b1[:].unsqueeze(1).to_broadcast([P, BG, PACK]),
-                        op0=MULT,
-                        op1=ADD,
-                    )
-                if qb is not None:
-                    ot = work.tile([P, O], F32, name="o_pre")
-                    nc.vector.tensor_tensor(out=ot[:], in0=o_ps[qb][:, :O], in1=b2[:], op=ADD)
-                    o_pre[qb] = ot
-                if g < GROUPS:
-                    evac_v(g, 3)
-                    qs = [0, 1] if PATHS[g][3] in "EA" or PATHS[g][2] in "CP" else [1, 0]
-                    if g < GROUPS - 1:
-                        quantize(g, qs[0])
-                if qa is not None:
-                    m1 = work.tile([P, BG, H, PACK], BF16, name="m1", align_bytes=64)
-                    nc.vector.tensor_scalar(
-                        out=m1[:],
-                        in0=pre[:].unsqueeze(2).to_broadcast([P, BG, H, PACK]),
-                        scalar1=0.0,
-                        scalar2=None,
-                        op0=MAX,
-                    )
-                if g == 0:
+                    o_ps[qb] = t
+                for s in vec[2:]:
+                    empty_and_scale(s)
+                for n in upcoming:
+                    scale_on_vector(n)
+                if r == 0:
                     for c in range(PASSES):
                         nc.vector.quantize_mx(
                             out=w1_codes[:, c, :].bitcast(FP8X4),
                             scales=w1_scales[:, c, :],
                             in_=w1_grouped[:, c].rearrange("p n t -> p (n t)"),
                         )
-                if g < GROUPS:
-                    quantize(g, qs[1])
-                if g == 0:
-                    nc.vector.tensor_copy(
-                        out=scale_perm[:].rearrange("p (u n e) -> p u n e", u=2, e=2),
-                        in_=scale_nat[:].rearrange("p (n u e) -> p u n e", u=2, e=2),
-                    )
+                if r == 2:
+                    nc.vector.quantize_mx(out=w2_codes[:].bitcast(FP8X4), scales=w2_scales[:], in_=w2_grouped[:])
+                todo = ORDER[r] if live else []
+                for pair in todo[:-1]:
+                    quantize(pair)
+                for n in upcoming:
+                    token(n)
+                for pair in todo[-1:]:
+                    quantize(pair)
                 if qa is not None:
-                    mc = work.tile([P, P], U32, name="m1_codes", align_bytes=64)
-                    ms = work.tile([P, P], U8, name="m1_scales", align_bytes=64)
-                    nc.vector.quantize_mx(
-                        out=mc[:].bitcast(FP8X4), scales=ms[:], in_=m1[:].rearrange("p b h t -> p (b h t)")
+                    t = work.tile([P, BG, PACK], F32, name="m1_pre")
+                    nc.vector.scalar_tensor_tensor(
+                        out=t[:],
+                        in0=m1_ps[qa][:, : PACK * BG].rearrange("p (t b) -> p b t", t=PACK),
+                        scalar=1.0 / NODES,
+                        in1=b1[:].unsqueeze(1).to_broadcast([P, BG, PACK]),
+                        op0=MULT,
+                        op1=ADD,
                     )
-                    m1_codes[qa], m1_scales[qa] = mc, ms
+                    m1_pre[qa] = t
+                if qb is not None:
+                    t = work.tile([P, O], F32, name="o_pre")
+                    nc.vector.tensor_tensor(out=t[:], in0=o_ps[qb][:, :O], in1=b2[:], op=ADD)
+                    o_pre[qb] = t
+                if r == 1:
+                    bank = turn_psum.tile([P, 512], F32, name="bank")
+                    words = w2[:].bitcast(F32)
+                    for u in range(2):
+                        nc.tensor.transpose(bank[:, u * P : (u + 1) * P], words[:, u:256:2], ident[:])
+                    nc.scalar.copy(
+                        out=w2_grouped[:].bitcast(F32).rearrange("p (n u) -> p n u", u=2),
+                        in_=bank[:, : 2 * P].rearrange("p (u n) -> p n u", u=2),
+                    )
+                for n in upcoming:
+                    widen(n)
+                    prepared = n + 1
+                if qm is not None:
+                    t = work.tile([P, G], F32, name="acc_copy")
+                    for i in range(2):
+                        part = slice(i * G // 2, (i + 1) * G // 2)
+                        nc.scalar.copy(out=t[:, part], in_=accs[qm][:, part])
+                    acc_sb[qm] = t
                 if qb is not None:
                     rows = work.tile([P, REPS, O], F32, name="out_rows")
-                    nc.scalar.activation(
-                        out=rows[:], in_=o_pre[qb][:].unsqueeze(1).to_broadcast([P, REPS, O]), func=RELU
-                    )
+                    spread = o_pre[qb][:].unsqueeze(1).to_broadcast([P, REPS, O])
+                    if qb == BATCHES - 1:
+                        nc.vector.tensor_scalar(out=rows[:], in0=spread, scalar1=0.0, scalar2=None, op0=MAX)
+                    else:
+                        nc.scalar.activation(out=rows[:], in_=spread, func=RELU)
                     nc.sync.dma_start(
                         out=out_view[qb].rearrange("p (a n) -> p a n", n=REPS * O),
                         in_=rows[:]
@@ -311,27 +361,3 @@ def tile_gcn_pa_t_kernel(tc, x_bytes, x_scale, W1g, b1g, W2g, b2g, out):
                         .unsqueeze(1)
                         .to_broadcast([P, SLOTS // REPS, REPS * O]),
                     )
-                if g == 1:
-                    bank = turn_psum.tile([P, 512], F32, name="bank")
-                    words = w2[:].bitcast(F32)
-                    for u in range(2):
-                        nc.tensor.transpose(bank[:, u * P : (u + 1) * P], words[:, u:256:2], ident[:])
-                    nc.vector.tensor_copy(
-                        out=w2_grouped[:].rearrange("p n t -> p (n t)").bitcast(F32).rearrange("p (n u) -> p n u", u=2),
-                        in_=bank[:, : 2 * P].rearrange("p (u n) -> p n u", u=2),
-                    )
-                    nc.vector.quantize_mx(
-                        out=w2_codes[:].bitcast(FP8X4),
-                        scales=w2_scales[:],
-                        in_=w2_grouped[:].rearrange("p n t -> p (n t)"),
-                    )
-                if g + AHEAD < GROUPS:
-                    widen(g + AHEAD)
-                    widen_v(g + AHEAD)
-                if g >= GPB and g % GPB == 0:
-                    q = g // GPB - 1
-                    at = work.tile([P, G], F32, name="acc_copy")
-                    for i in range(2):
-                        part = slice(i * G // 2, (i + 1) * G // 2)
-                        nc.scalar.copy(out=at[:, part], in_=accs[q][:, part])
-                    acc_sb[q] = at

@@ -21,44 +21,46 @@ P = 128
 PACK = 4
 PASSES = F // (P * PACK)
 BATCHES = 4
-BG = GRAPHS // BATCHES
-H = P // BG
-SLOTS = NODES // H
-CHUNK = 4
+BATCH_GRAPHS = GRAPHS // BATCHES
+SHARE = P // BATCH_GRAPHS
+SLABS = NODES // SHARE
+RUN = 4
+RUNS = BATCHES * SLABS // RUN
+BATCH_RUNS = SLABS // RUN
 LOADS = 7
-REPS = 4
+COPIES = 4
 
-RUNS = ["CCCC", "CCCC"] + ["CCCE", "CCAE"] * 7
-FIRST = [sum(len(run) for run in RUNS[:r]) for r in range(len(RUNS))]
-KIND = "".join(RUNS)
-LOOK = 8
+ROLES = ["VVVV", "WVVV"] + ["GWVV"] * (RUNS - 2)
 
 
 def tile_gcn_pa_t_kernel(tc, x_bytes, x_scale, W1g, b1g, W2g, b2g, out):
     nc = tc.nc
-    x_view = x_bytes.rearrange("(q b) (h c) d f -> q (b h) (c d f)", q=BATCHES, h=H)
-    out_view = out.rearrange("(q b) (h s) o -> q (b h) (s o)", q=BATCHES, h=H)
+    x_view = x_bytes.rearrange("(q b) (h c) d f -> q (b h) (c d f)", q=BATCHES, h=SHARE)
+    out_view = out.rearrange("(q b) (h s) o -> q (b h) (s o)", q=BATCHES, h=SHARE)
     scale_row = x_scale.rearrange("a b c f -> (a b c f)")
     w1_view = W1g.rearrange("(p t) k -> p t k", t=PACK)
 
     with ExitStack() as ctx:
         const = ctx.enter_context(tc.tile_pool(name="const", bufs=1))
         bytes_pool = ctx.enter_context(tc.tile_pool(name="bytes_pool", bufs=LOADS + 1))
-        wide_pool = ctx.enter_context(tc.tile_pool(name="wide_pool", bufs=16))
-        scaled_pool = ctx.enter_context(tc.tile_pool(name="scaled_pool", bufs=16))
+        wide_pool = ctx.enter_context(tc.tile_pool(name="wide_pool", bufs=24))
+        sorted_pool = ctx.enter_context(tc.tile_pool(name="sorted_pool", bufs=24))
         grouped_pool = ctx.enter_context(tc.tile_pool(name="grouped_pool", bufs=6))
         code_pool = ctx.enter_context(tc.tile_pool(name="code_pool", bufs=8))
         work = ctx.enter_context(tc.tile_pool(name="work", bufs=2))
         turn_psum = ctx.enter_context(tc.psum_pool(name="turn_psum", bufs=5))
-        acc_psum = ctx.enter_context(tc.psum_pool(name="acc_psum", bufs=2))
+        sum_psum = ctx.enter_context(tc.psum_pool(name="sum_psum", bufs=2))
         small_psum = ctx.enter_context(tc.psum_pool(name="small_psum", bufs=1))
 
         ident = const.tile([P, P], F32, name="ident")
-        scale_t = const.tile([P, PASSES, PACK], F32, name="scale_t")
-        scale_nat = const.tile([P, F], F32, name="scale_nat")
-        scale_perm = const.tile([P, F], F32, name="scale_perm")
+        scale_turned = const.tile([P, PASSES, PACK], F32, name="scale_turned")
+        scale_plain = const.tile([P, F], F32, name="scale_plain")
+        scale_sorted = const.tile([P, F], F32, name="scale_sorted")
         w1 = const.tile([P, PACK, F], BF16, name="w1")
-        w1_grouped = const.tile([P, PASSES, G, PACK], BF16, name="w1_grouped", align_bytes=64)
+        w1_grouped = []
+        for t in range(PACK):
+            w1_part = const.tile([P, PASSES, P * PACK], BF16, name="w1_grouped_%d" % t, align_bytes=64)
+            w1_grouped.append(w1_part)
         w1_codes = const.tile([P, PASSES, G], U32, name="w1_codes", align_bytes=64)
         w1_scales = const.tile([P, PASSES, G], U8, name="w1_scales", align_bytes=64)
         w2 = const.tile([P, G], BF16, name="w2")
@@ -67,92 +69,85 @@ def tile_gcn_pa_t_kernel(tc, x_bytes, x_scale, W1g, b1g, W2g, b2g, out):
         w2_scales = const.tile([P, O], U8, name="w2_scales", align_bytes=64)
         b1 = const.tile([P, PACK], BF16, name="b1")
         b2 = const.tile([P, O], BF16, name="b2")
-        pick = const.tile([P, BG], F32, name="pick")
+        same_graph = const.tile([P, BATCH_GRAPHS], F32, name="same_graph")
 
-        chunks, ready, tokened, turned, grouped, codes, scales = {}, {}, {}, {}, {}, {}, {}
-        accs, acc_sb, m1_ps, m1_pre, o_ps, o_pre = {}, {}, {}, {}, {}, {}
+        x_in, wide, ready, turned, grouped, codes, scales = {}, {}, {}, {}, {}, {}, {}
+        sums, sums_copy, hidden_psum, hidden, out_psum, out_sum = {}, {}, {}, {}, {}, {}
 
-        def load(chunk, split=1):
-            t = bytes_pool.tile([P, CHUNK * F], U8, name="x_in")
-            q, at = divmod(chunk * CHUNK, SLOTS)
-            n = CHUNK * F // split
-            for i in range(split):
-                nc.sync.dma_start(
-                    out=t[:, i * n : (i + 1) * n], in_=x_view[q, :, at * F + i * n : at * F + (i + 1) * n]
+        def slabs_of(r, roles):
+            return [r * RUN + i for i in range(RUN) if ROLES[r][i] in roles]
+
+        def load(r, pieces=1):
+            t = bytes_pool.tile([P, RUN * F], U8, name="x_in")
+            q, i = divmod(r, BATCH_RUNS)
+            n = RUN * F // pieces
+            for j in range(pieces):
+                at = i * RUN * F + j * n
+                nc.sync.dma_start(out=t[:, j * n : (j + 1) * n], in_=x_view[q, :, at : at + n])
+            x_in[r] = t
+
+        def widen(r, roles):
+            for role in roles:
+                for s in slabs_of(r, role):
+                    t = wide_pool.tile([P, F], BF16, name="x_wide")
+                    nc.scalar.copy(out=t[:], in_=x_in[r][:, s % RUN * F : (s % RUN + 1) * F].bitcast(FP8))
+                    wide[s] = t
+                    ready[s] = t
+            for s in slabs_of(r, "W") if "W" in roles else []:
+                t = sorted_pool.tile([P, F], BF16, name="x_sorted")
+                nc.scalar.copy(
+                    out=t[:].bitcast(F32).rearrange("p (u n) -> p u n", u=2),
+                    in_=wide[s][:].bitcast(F32).rearrange("p (n u) -> p u n", u=2),
                 )
-            chunks[chunk] = t
-
-        def slot_bytes(s):
-            return chunks[s // CHUNK][:, s % CHUNK * F : (s % CHUNK + 1) * F].bitcast(FP8)
-
-        def slots_of(r, kinds):
-            return [s for s in range(FIRST[r], FIRST[r] + len(RUNS[r])) if KIND[s] in kinds]
-
-        def token(r):
-            for s in slots_of(r, "E"):
-                t = scaled_pool.tile([P, F], BF16, name="x_scaled")
-                nc.vector.memset(t[:, 0:2], 0.0)
-                tokened[s] = t
-
-        def scale_on_vector(r):
-            for s in slots_of(r, "A"):
-                t = scaled_pool.tile([P, F], BF16, name="x_scaled")
-                nc.vector.tensor_tensor(out=t[:], in0=slot_bytes(s), in1=scale_nat[:], op=MULT)
                 ready[s] = t
 
-        def widen(r):
-            for s in slots_of(r, "E") + slots_of(r, "PC"):
-                wide = wide_pool.tile([P, F], BF16, name="x_wide")
-                nc.scalar.copy(out=wide[:], in_=slot_bytes(s))
-                ready[s] = wide
-                if KIND[s] == "P":
-                    t = scaled_pool.tile([P, F], BF16, name="x_scaled")
-                    nc.scalar.copy(
-                        out=t[:].bitcast(F32).rearrange("p (u n) -> p u n", u=2),
-                        in_=wide[:].bitcast(F32).rearrange("p (n u) -> p u n", u=2),
-                    )
-                    ready[s] = t
-                if KIND[s] == "E":
-                    t = tokened[s]
-                    for u in range(2):
-                        half = slice(u * F // 2, (u + 1) * F // 2)
-                        nc.gpsimd.tensor_tensor(
-                            out=t[:, half].rearrange("p (n e) -> p n e", e=2),
-                            in0=wide[:].rearrange("p (n u e) -> p u n e", u=2, e=2)[:, u],
-                            in1=scale_perm[:, half].rearrange("p (n e) -> p n e", e=2),
-                            op=MULT,
-                        )
-                    ready[s] = t
+        def hold_gpsimd(r):
+            for s in slabs_of(r, "G"):
+                t = sorted_pool.tile([P, F], BF16, name="x_sorted")
+                nc.vector.memset(t[:, 0:2], 0.0)
+                ready[s] = t
+
+        def scale_on_gpsimd(r):
+            for s in slabs_of(r, "G"):
+                nc.gpsimd.tensor_tensor(
+                    out=ready[s][:].rearrange("p (u n e) -> p u n e", u=2, e=2),
+                    in0=wide[s][:].rearrange("p (n u e) -> p u n e", u=2, e=2),
+                    in1=scale_sorted[:].rearrange("p (u n e) -> p u n e", u=2, e=2),
+                    op=MULT,
+                )
 
         def turn(rows, in_order):
-            bank = turn_psum.tile([P, 512], F32, name="bank")
+            bank = turn_psum.tile([P, F // 2], F32, name="bank")
             words = rows.bitcast(F32)
             for u in range(2):
                 for c in range(PASSES):
                     at = (u * PASSES + c) * P
-                    cols = slice(at, at + P) if in_order else slice(256 * c + u, 256 * (c + 1), 2)
+                    cols = slice(at, at + P) if in_order else slice(2 * P * c + u, 2 * P * (c + 1), 2)
                     nc.tensor.transpose(bank[:, at : at + P], words[:, cols], ident[:])
             return bank
 
-        def half_of(s):
-            pair = s // 2
-            if pair not in grouped:
-                t = grouped_pool.tile([P, 2 * F], BF16, name="x_grouped", align_bytes=64)
-                grouped[pair] = t
-            return grouped[pair][:, s % 2 * F : (s % 2 + 1) * F]
+        def turn_run(r):
+            for s in slabs_of(r, "VW") + slabs_of(r, "G"):
+                bank = turn(ready[s][:], ROLES[r][s % RUN] in "GW")
+                turned[s] = bank
 
-        def empty_on_scalar(r):
-            for s in slots_of(r, "AE"):
-                nc.scalar.copy(
-                    out=half_of(s).bitcast(F32).rearrange("p (n u) -> p n u", u=2),
-                    in_=turned[s][:].rearrange("p (u n) -> p n u", u=2),
-                )
+        def grouped_half(s):
+            if s // 2 not in grouped:
+                t = grouped_pool.tile([P, 2 * F], BF16, name="x_grouped", align_bytes=64)
+                grouped[s // 2] = t
+            return grouped[s // 2][:, s % 2 * F : (s % 2 + 1) * F]
+
+        def empty(s):
+            nc.scalar.copy(
+                out=grouped_half(s).bitcast(F32).rearrange("p (n u) -> p n u", u=2),
+                in_=turned[s][:].rearrange("p (u n) -> p n u", u=2),
+            )
 
         def empty_and_scale(s):
             nc.vector.tensor_tensor(
-                out=half_of(s).rearrange("p (c r u e) -> p c r u e", c=PASSES, u=2, e=2),
+                out=grouped_half(s).rearrange("p (c r u e) -> p c r u e", c=PASSES, u=2, e=2),
                 in0=turned[s][:].bitcast(BF16).rearrange("p (u c r e) -> p c r u e", u=2, c=PASSES, e=2),
-                in1=scale_t[:]
+                in1=scale_turned[:]
                 .rearrange("p c (u e) -> p c u e", u=2)
                 .unsqueeze(2)
                 .to_broadcast([P, PASSES, P, 2, 2]),
@@ -160,204 +155,215 @@ def tile_gcn_pa_t_kernel(tc, x_bytes, x_scale, W1g, b1g, W2g, b2g, out):
             )
 
         def quantize(pair):
-            ct = code_pool.tile([P, 2 * PASSES * P], U32, name="x_codes", align_bytes=64)
-            st = code_pool.tile([P, 2 * PASSES * P], U8, name="x_scales", align_bytes=64)
-            nc.vector.quantize_mx(out=ct[:].bitcast(FP8X4), scales=st[:], in_=grouped[pair][:])
-            codes[pair], scales[pair] = ct, st
-
-        def pairs_of(r):
-            pairs = [s // 2 for s in slots_of(r, "ACEP") if s % 2 == 0]
-            return pairs
+            pair_codes = code_pool.tile([P, 2 * PASSES * P], U32, name="x_codes", align_bytes=64)
+            pair_scales = code_pool.tile([P, 2 * PASSES * P], U8, name="x_scales", align_bytes=64)
+            nc.vector.quantize_mx(out=pair_codes[:].bitcast(FP8X4), scales=pair_scales[:], in_=grouped[pair][:])
+            codes[pair], scales[pair] = pair_codes, pair_scales
 
         def multiply(r):
-            q = FIRST[r] // SLOTS
-            if FIRST[r] % SLOTS == 0:
-                t = acc_psum.tile([P, G], F32, name="acc")
-                accs[q] = t
-            for pair in ORDER[r]:
-                for i in range(2 * PASSES):
-                    cols = slice(i * P, (i + 1) * P)
+            q, i = divmod(r, BATCH_RUNS)
+            if i == 0:
+                t = sum_psum.tile([P, G], F32, name="sum")
+                sums[q] = t
+            for s in range(r * RUN, (r + 1) * RUN):
+                for c in range(PASSES):
+                    at = (s % 2 * PASSES + c) * P
                     nc.tensor.matmul_mx(
-                        out=accs[q][:],
-                        lhsT=codes[pair][:, cols].bitcast(FP8X4),
-                        lhsT_scale=scales[pair][:, cols],
-                        rhs=w1_codes[:, i % PASSES, :].bitcast(FP8X4),
-                        rhs_scale=w1_scales[:, i % PASSES, :],
-                        start=(FIRST[r] % SLOTS == 0 and pair == ORDER[r][0] and i == 0),
-                        stop=((FIRST[r] + len(RUNS[r])) % SLOTS == 0 and pair == ORDER[r][-1] and i == 2 * PASSES - 1),
+                        out=sums[q][:],
+                        lhsT=codes[s // 2][:, at : at + P].bitcast(FP8X4),
+                        lhsT_scale=scales[s // 2][:, at : at + P],
+                        rhs=w1_codes[:, c, :].bitcast(FP8X4),
+                        rhs_scale=w1_scales[:, c, :],
+                        start=(s % SLABS == 0 and c == 0),
+                        stop=(s % SLABS == SLABS - 1 and c == PASSES - 1),
                     )
 
-        def prepare_w1(t):
-            bank = turn(w1[:, t, :], False)
-            nc.vector.tensor_copy(
-                out=w1_grouped[:, :, t * P : (t + 1) * P, :]
-                .rearrange("p c n t -> p c (n t)")
-                .bitcast(F32)
-                .rearrange("p c (n u) -> p c n u", u=2),
-                in_=bank[:].rearrange("p (u c n) -> p c n u", u=2, c=PASSES),
+        def turn_weights():
+            for t in range(PACK):
+                bank = turn(w1[:, t, :], False)
+                nc.scalar.copy(
+                    out=w1_grouped[t][:].bitcast(F32).rearrange("p c (n u) -> p c n u", u=2),
+                    in_=bank[:].rearrange("p (u c n) -> p c n u", u=2, c=PASSES),
+                )
+            bank = turn_psum.tile([P, F // 2], F32, name="bank")
+            words = w2[:].bitcast(F32)
+            for u in range(2):
+                nc.tensor.transpose(bank[:, u * P : (u + 1) * P], words[:, u : 2 * P : 2], ident[:])
+            nc.scalar.copy(
+                out=w2_grouped[:].bitcast(F32).rearrange("p (n u) -> p n u", u=2),
+                in_=bank[:, : 2 * P].rearrange("p (u n) -> p n u", u=2),
             )
 
-        for t in range(2):
-            nc.sync.dma_start(out=w1[:, t, :], in_=w1_view[:, t, :])
-        load(0, 2)
-        for t in range(2, 4):
-            nc.sync.dma_start(out=w1[:, t, :], in_=w1_view[:, t, :])
-        nc.sync.dma_start(out=scale_t[:], in_=scale_row.rearrange("(c p t) -> p c t", c=PASSES, t=PACK))
+        def quantize_w1():
+            for t in range(PACK):
+                for c in range(PASSES):
+                    nc.vector.quantize_mx(
+                        out=w1_codes[:, c, t * P : (t + 1) * P].bitcast(FP8X4),
+                        scales=w1_scales[:, c, t * P : (t + 1) * P],
+                        in_=w1_grouped[t][:, c],
+                    )
+
+
+        def copy_sums(q):
+            t = work.tile([P, G], F32, name="sums_copy")
+            for i in range(2):
+                part = slice(i * G // 2, (i + 1) * G // 2)
+                nc.scalar.copy(out=t[:, part], in_=sums[q][:, part])
+            sums_copy[q] = t
+
+        def add_shares(q):
+            t = small_psum.tile([P, G], F32, name="small")
+            for i in range(PACK):
+                nc.tensor.matmul(
+                    t[:, i * BATCH_GRAPHS : (i + 1) * BATCH_GRAPHS],
+                    lhsT=sums_copy[q][:, i * P : (i + 1) * P],
+                    rhs=same_graph[:],
+                    start=True,
+                    stop=True,
+                )
+            hidden_psum[q] = t
+
+        def mean_and_bias(q):
+            t = work.tile([P, BATCH_GRAPHS, PACK], F32, name="hidden")
+            nc.vector.scalar_tensor_tensor(
+                out=t[:],
+                in0=hidden_psum[q][:, : PACK * BATCH_GRAPHS].rearrange("p (t b) -> p b t", t=PACK),
+                scalar=1.0 / NODES,
+                in1=b1[:].unsqueeze(1).to_broadcast([P, BATCH_GRAPHS, PACK]),
+                op0=MULT,
+                op1=ADD,
+            )
+            hidden[q] = t
+
+        def relu_rounded(q):
+            t = work.tile([P, BATCH_GRAPHS, SHARE, PACK], BF16, name="m1", align_bytes=64)
+            spread = hidden[q][:].unsqueeze(2).to_broadcast([P, BATCH_GRAPHS, SHARE, PACK])
+            if q == BATCHES - 1:
+                nc.vector.tensor_scalar(out=t[:], in0=spread, scalar1=0.0, scalar2=None, op0=MAX)
+            else:
+                nc.scalar.activation(out=t[:], in_=spread, func=RELU)
+            return t
+
+        def second_layer(q, m1):
+            m1_codes = work.tile([P, P], U32, name="m1_codes", align_bytes=64)
+            m1_scales = work.tile([P, P], U8, name="m1_scales", align_bytes=64)
+            nc.vector.quantize_mx(
+                out=m1_codes[:].bitcast(FP8X4), scales=m1_scales[:], in_=m1[:].rearrange("p b h t -> p (b h t)")
+            )
+            t = small_psum.tile([P, G], F32, name="small")
+            nc.tensor.matmul_mx(
+                out=t[:, :O],
+                lhsT=m1_codes[:].bitcast(FP8X4),
+                lhsT_scale=m1_scales[:],
+                rhs=w2_codes[:].bitcast(FP8X4),
+                rhs_scale=w2_scales[:],
+                start=True,
+                stop=True,
+            )
+            out_psum[q] = t
+
+        def add_b2(q):
+            t = work.tile([P, O], F32, name="out_sum")
+            nc.vector.tensor_tensor(out=t[:], in0=out_psum[q][:, :O], in1=b2[:], op=ADD)
+            out_sum[q] = t
+
+        def store(q):
+            t = work.tile([P, COPIES, O], F32, name="out_rows")
+            spread = out_sum[q][:].unsqueeze(1).to_broadcast([P, COPIES, O])
+            if q == BATCHES - 1:
+                nc.vector.tensor_scalar(out=t[:], in0=spread, scalar1=0.0, scalar2=None, op0=MAX)
+            else:
+                nc.scalar.activation(out=t[:], in_=spread, func=RELU)
+            nc.sync.dma_start(
+                out=out_view[q].rearrange("p (a n) -> p a n", n=COPIES * O),
+                in_=t[:].rearrange("p r o -> p (r o)").unsqueeze(1).to_broadcast([P, SLABS // COPIES, COPIES * O]),
+            )
+
+        load(0, RUN)
+        nc.sync.dma_start(out=scale_turned[:], in_=scale_row.rearrange("(c p t) -> p c t", c=PASSES, t=PACK))
         load(1)
-        nc.sync.dma_start(out=scale_nat[:], in_=scale_row.partition_broadcast(P))
+        for t in range(PACK):
+            nc.sync.dma_start(out=w1[:, t, :], in_=w1_view[:, t, :])
         nc.sync.dma_start(out=w2[:], in_=W2g)
+        nc.sync.dma_start(out=scale_plain[:], in_=scale_row.partition_broadcast(P))
         nc.sync.dma_start(out=b1[:], in_=b1g.rearrange("(p t) -> p t", t=PACK))
         nc.sync.dma_start(out=b2[:], in_=b2g.partition_broadcast(P))
-        for chunk in range(2, LOADS):
-            load(chunk)
+        for r in range(2, LOADS):
+            load(r)
         make_identity(nc, ident[:])
         nc.vector.tensor_reduce(
-            out=pick[:], in_=ident[:].rearrange("p (b h) -> p b h", h=H), axis=mybir.AxisListType.X, op=ADD
+            out=same_graph[:],
+            in_=ident[:].rearrange("p (b h) -> p b h", h=SHARE),
+            axis=mybir.AxisListType.X,
+            op=ADD,
         )
-        nc.gpsimd.tensor_copy(
-            out=scale_perm[:].rearrange("p (u n e) -> p u n e", u=2, e=2),
-            in_=scale_nat[:].rearrange("p (n u e) -> p u n e", u=2, e=2),
-        )
-
-        last_run = len(RUNS) - 1
-        ORDER = {}
-        for r in range(len(RUNS)):
-            vec = [p for p in pairs_of(r) if KIND[2 * p] in "CP" or KIND[2 * p + 1] in "CP"]
-            sca = [p for p in pairs_of(r) if p not in vec]
-            ORDER[r] = sca + vec if r >= last_run - 1 else vec + sca
-        ends = [r for r in range(len(RUNS)) if (FIRST[r] + len(RUNS[r])) % SLOTS == 0]
 
         with tc.manual_schedule():
-            prepared = 0
-            loaded = LOADS
+            for r in range(RUNS + 3):
+                live = r < RUNS
+                by_vector = slabs_of(r, "VW") if live else []
+                pairs = [r * RUN // 2 + i for i in range(RUN // 2)] if live else []
+                summed, shared, finished = [
+                    (r - d) // BATCH_RUNS if r >= d and (r - d) % BATCH_RUNS == BATCH_RUNS - 1 else None
+                    for d in (1, 2, 3)
+                ]
 
-            for r in range(len(RUNS) + 3):
-                live = r < len(RUNS)
-                qm = ends.index(r - 1) if r - 1 in ends else None
-                qa = ends.index(r - 2) if r - 2 in ends else None
-                qb = ends.index(r - 3) if r - 3 in ends else None
-                end = FIRST[r] + len(RUNS[r]) if live else len(KIND)
-                upcoming = [n for n in range(prepared, len(RUNS)) if FIRST[n] < end + LOOK]
                 if r == 0:
-                    for n in upcoming[:2]:
-                        token(n)
-                        scale_on_vector(n)
-                        widen(n)
-                    prepared = 2
-                    upcoming = upcoming[2:]
-                    for t in range(PACK):
-                        prepare_w1(t)
-                if loaded * CHUNK < len(KIND) and loaded * CHUNK < end + LOADS * CHUNK:
-                    load(loaded)
-                    loaded += 1
-                vec = slots_of(r, "CP") if live else []
+                    widen(0, "V")
+                if r + LOADS < RUNS:
+                    load(r + LOADS)
                 if live:
-                    for s in slots_of(r, "A") + slots_of(r, "CP") + slots_of(r, "E"):
-                        bank = turn(ready[s][:], KIND[s] in "EP")
-                        turned[s] = bank
-                    empty_on_scalar(r)
-                for s in vec[:1]:
-                    empty_and_scale(s)
-                if qb is not None:
-                    m1 = work.tile([P, BG, H, PACK], BF16, name="m1", align_bytes=64)
-                    spread = m1_pre[qb][:].unsqueeze(2).to_broadcast([P, BG, H, PACK])
-                    nc.vector.tensor_scalar(out=m1[:], in0=spread, scalar1=0.0, scalar2=None, op0=MAX)
-                if 1 <= r <= len(RUNS):
-                    multiply(r - 1)
-                if qa is not None:
-                    t = small_psum.tile([P, 512], F32, name="small")
-                    for i in range(PACK):
-                        nc.tensor.matmul(
-                            t[:, i * BG : (i + 1) * BG],
-                            lhsT=acc_sb[qa][:, i * P : (i + 1) * P],
-                            rhs=pick[:],
-                            start=True,
-                            stop=True,
-                        )
-                    m1_ps[qa] = t
-                for s in vec[1:2]:
-                    empty_and_scale(s)
-                if qb is not None:
-                    mc = work.tile([P, P], U32, name="m1_codes", align_bytes=64)
-                    ms = work.tile([P, P], U8, name="m1_scales", align_bytes=64)
-                    nc.vector.quantize_mx(
-                        out=mc[:].bitcast(FP8X4), scales=ms[:], in_=m1[:].rearrange("p b h t -> p (b h t)")
-                    )
-                    t = small_psum.tile([P, 512], F32, name="small")
-                    nc.tensor.matmul_mx(
-                        out=t[:, :O],
-                        lhsT=mc[:].bitcast(FP8X4),
-                        lhsT_scale=ms[:],
-                        rhs=w2_codes[:].bitcast(FP8X4),
-                        rhs_scale=w2_scales[:],
-                        start=True,
-                        stop=True,
-                    )
-                    o_ps[qb] = t
-                for s in vec[2:]:
-                    empty_and_scale(s)
-                for n in upcoming:
-                    scale_on_vector(n)
+                    turn_run(r)
+                    for s in slabs_of(r, "G"):
+                        empty(s)
                 if r == 0:
-                    for c in range(PASSES):
-                        nc.vector.quantize_mx(
-                            out=w1_codes[:, c, :].bitcast(FP8X4),
-                            scales=w1_scales[:, c, :],
-                            in_=w1_grouped[:, c].rearrange("p n t -> p (n t)"),
-                        )
+                    widen(1, "WV")
+                    turn_weights()
+                for s in by_vector[:1]:
+                    empty_and_scale(s)
+                if finished is not None:
+                    m1 = relu_rounded(finished)
+                for s in by_vector[1:2]:
+                    empty_and_scale(s)
+                if r == 1:
+                    quantize_w1()
+                    hold_gpsimd(2)
+                    scale_on_gpsimd(2)
+                if 1 <= r <= RUNS:
+                    multiply(r - 1)
+                if shared is not None:
+                    add_shares(shared)
+                if finished is not None:
+                    second_layer(finished, m1)
+                if r == RUNS - 1:
+                    quantize(pairs[0])
+                for s in by_vector[2:]:
+                    empty_and_scale(s)
+                if r == 0:
+                    nc.vector.tensor_copy(
+                        out=scale_sorted[:].rearrange("p (u n e) -> p u n e", u=2, e=2),
+                        in_=scale_plain[:].rearrange("p (n u e) -> p u n e", u=2, e=2),
+                    )
                 if r == 2:
                     nc.vector.quantize_mx(out=w2_codes[:].bitcast(FP8X4), scales=w2_scales[:], in_=w2_grouped[:])
-                todo = ORDER[r] if live else []
-                for pair in todo[:-1]:
-                    quantize(pair)
-                for n in upcoming:
-                    token(n)
-                for pair in todo[-1:]:
-                    quantize(pair)
-                if qa is not None:
-                    t = work.tile([P, BG, PACK], F32, name="m1_pre")
-                    nc.vector.scalar_tensor_tensor(
-                        out=t[:],
-                        in0=m1_ps[qa][:, : PACK * BG].rearrange("p (t b) -> p b t", t=PACK),
-                        scalar=1.0 / NODES,
-                        in1=b1[:].unsqueeze(1).to_broadcast([P, BG, PACK]),
-                        op0=MULT,
-                        op1=ADD,
-                    )
-                    m1_pre[qa] = t
-                if qb is not None:
-                    t = work.tile([P, O], F32, name="o_pre")
-                    nc.vector.tensor_tensor(out=t[:], in0=o_ps[qb][:, :O], in1=b2[:], op=ADD)
-                    o_pre[qb] = t
-                if r == 1:
-                    bank = turn_psum.tile([P, 512], F32, name="bank")
-                    words = w2[:].bitcast(F32)
-                    for u in range(2):
-                        nc.tensor.transpose(bank[:, u * P : (u + 1) * P], words[:, u:256:2], ident[:])
-                    nc.scalar.copy(
-                        out=w2_grouped[:].bitcast(F32).rearrange("p (n u) -> p n u", u=2),
-                        in_=bank[:, : 2 * P].rearrange("p (u n) -> p n u", u=2),
-                    )
-                for n in upcoming:
-                    widen(n)
-                    prepared = n + 1
-                if qm is not None:
-                    t = work.tile([P, G], F32, name="acc_copy")
-                    for i in range(2):
-                        part = slice(i * G // 2, (i + 1) * G // 2)
-                        nc.scalar.copy(out=t[:, part], in_=accs[qm][:, part])
-                    acc_sb[qm] = t
-                if qb is not None:
-                    rows = work.tile([P, REPS, O], F32, name="out_rows")
-                    spread = o_pre[qb][:].unsqueeze(1).to_broadcast([P, REPS, O])
-                    if qb == BATCHES - 1:
-                        nc.vector.tensor_scalar(out=rows[:], in0=spread, scalar1=0.0, scalar2=None, op0=MAX)
-                    else:
-                        nc.scalar.activation(out=rows[:], in_=spread, func=RELU)
-                    nc.sync.dma_start(
-                        out=out_view[qb].rearrange("p (a n) -> p a n", n=REPS * O),
-                        in_=rows[:]
-                        .rearrange("p r o -> p (r o)")
-                        .unsqueeze(1)
-                        .to_broadcast([P, SLOTS // REPS, REPS * O]),
-                    )
+                if r < RUNS - 1:
+                    quantize(pairs[0])
+                if 1 <= r < RUNS - 2:
+                    hold_gpsimd(r + 2)
+                if live:
+                    quantize(pairs[1])
+                if shared is not None:
+                    mean_and_bias(shared)
+                if finished is not None:
+                    add_b2(finished)
+                if 1 <= r < RUNS - 2:
+                    scale_on_gpsimd(r + 2)
+                for n in [2, 3] if r == 0 else [r + 3]:
+                    if n < RUNS:
+                        widen(n, "G")
+                if r + 2 < RUNS:
+                    widen(r + 2, "WV")
+                if summed is not None:
+                    copy_sums(summed)
+                if finished is not None:
+                    store(finished)

from contextlib import ExitStack

import concourse.mybir as mybir
from concourse.masks import make_identity

GRAPHS, NODES, F, G, O = 128, 64, 1024, 512, 128
FLOPS = 2 * GRAPHS * NODES * F * G + 2 * GRAPHS * G * O

F32 = mybir.dt.float32
BF16 = mybir.dt.bfloat16
U32 = mybir.dt.uint32
U8 = mybir.dt.uint8
FP8 = mybir.dt.float8_e4m3fn
FP8X4 = mybir.dt.float8_e4m3fn_x4
MULT = mybir.AluOpType.mult
ADD = mybir.AluOpType.add
MAX = mybir.AluOpType.max
RELU = mybir.ActivationFunctionType.Relu

P = 128
PACK = 4
PASSES = F // (P * PACK)
BATCHES = 4
BATCH_GRAPHS = GRAPHS // BATCHES
SHARE = P // BATCH_GRAPHS
SLABS = NODES // SHARE
RUN = 4
RUNS = BATCHES * SLABS // RUN
BATCH_RUNS = SLABS // RUN
LOADS = 7
COPIES = 4

ROLES = ["VVVV", "WVVV"] + ["GWVV"] * (RUNS - 2)


def tile_gcn_pa_t_kernel(tc, x_bytes, x_scale, W1g, b1g, W2g, b2g, out):
    nc = tc.nc
    x_view = x_bytes.rearrange("(q b) (h c) d f -> q (b h) (c d f)", q=BATCHES, h=SHARE)
    out_view = out.rearrange("(q b) (h s) o -> q (b h) (s o)", q=BATCHES, h=SHARE)
    scale_row = x_scale.rearrange("a b c f -> (a b c f)")
    w1_view = W1g.rearrange("(p t) k -> p t k", t=PACK)

    with ExitStack() as ctx:
        const = ctx.enter_context(tc.tile_pool(name="const", bufs=1))
        bytes_pool = ctx.enter_context(tc.tile_pool(name="bytes_pool", bufs=LOADS + 1))
        wide_pool = ctx.enter_context(tc.tile_pool(name="wide_pool", bufs=24))
        sorted_pool = ctx.enter_context(tc.tile_pool(name="sorted_pool", bufs=24))
        grouped_pool = ctx.enter_context(tc.tile_pool(name="grouped_pool", bufs=6))
        code_pool = ctx.enter_context(tc.tile_pool(name="code_pool", bufs=8))
        work = ctx.enter_context(tc.tile_pool(name="work", bufs=2))
        turn_psum = ctx.enter_context(tc.psum_pool(name="turn_psum", bufs=5))
        sum_psum = ctx.enter_context(tc.psum_pool(name="sum_psum", bufs=2))
        small_psum = ctx.enter_context(tc.psum_pool(name="small_psum", bufs=1))

        ident = const.tile([P, P], F32, name="ident")
        scale_turned = const.tile([P, PASSES, PACK], F32, name="scale_turned")
        scale_plain = const.tile([P, F], F32, name="scale_plain")
        scale_sorted = const.tile([P, F], F32, name="scale_sorted")
        w1 = const.tile([P, PACK, F], BF16, name="w1")
        w1_grouped = []
        for t in range(PACK):
            w1_part = const.tile([P, PASSES, P * PACK], BF16, name="w1_grouped_%d" % t, align_bytes=64)
            w1_grouped.append(w1_part)
        w1_codes = const.tile([P, PASSES, G], U32, name="w1_codes", align_bytes=64)
        w1_scales = const.tile([P, PASSES, G], U8, name="w1_scales", align_bytes=64)
        w2 = const.tile([P, G], BF16, name="w2")
        w2_grouped = const.tile([P, O * PACK], BF16, name="w2_grouped", align_bytes=64)
        w2_codes = const.tile([P, O], U32, name="w2_codes", align_bytes=64)
        w2_scales = const.tile([P, O], U8, name="w2_scales", align_bytes=64)
        b1 = const.tile([P, PACK], BF16, name="b1")
        b2 = const.tile([P, O], BF16, name="b2")
        same_graph = const.tile([P, BATCH_GRAPHS], F32, name="same_graph")

        x_in, wide, ready, turned, grouped, codes, scales = {}, {}, {}, {}, {}, {}, {}
        sums, sums_copy, hidden_psum, hidden, out_psum, out_sum = {}, {}, {}, {}, {}, {}

        def slabs_of(r, roles):
            return [r * RUN + i for i in range(RUN) if ROLES[r][i] in roles]

        def load(r, pieces=1):
            t = bytes_pool.tile([P, RUN * F], U8, name="x_in")
            q, i = divmod(r, BATCH_RUNS)
            n = RUN * F // pieces
            for j in range(pieces):
                at = i * RUN * F + j * n
                nc.sync.dma_start(out=t[:, j * n : (j + 1) * n], in_=x_view[q, :, at : at + n])
            x_in[r] = t

        def widen(r, roles):
            for role in roles:
                for s in slabs_of(r, role):
                    t = wide_pool.tile([P, F], BF16, name="x_wide")
                    nc.scalar.copy(out=t[:], in_=x_in[r][:, s % RUN * F : (s % RUN + 1) * F].bitcast(FP8))
                    wide[s] = t
                    ready[s] = t
            for s in slabs_of(r, "W") if "W" in roles else []:
                t = sorted_pool.tile([P, F], BF16, name="x_sorted")
                nc.scalar.copy(
                    out=t[:].bitcast(F32).rearrange("p (u n) -> p u n", u=2),
                    in_=wide[s][:].bitcast(F32).rearrange("p (n u) -> p u n", u=2),
                )
                ready[s] = t

        def hold_gpsimd(r):
            for s in slabs_of(r, "G"):
                t = sorted_pool.tile([P, F], BF16, name="x_sorted")
                nc.vector.memset(t[:, 0:2], 0.0)
                ready[s] = t

        def scale_on_gpsimd(r):
            for s in slabs_of(r, "G"):
                nc.gpsimd.tensor_tensor(
                    out=ready[s][:].rearrange("p (u n e) -> p u n e", u=2, e=2),
                    in0=wide[s][:].rearrange("p (n u e) -> p u n e", u=2, e=2),
                    in1=scale_sorted[:].rearrange("p (u n e) -> p u n e", u=2, e=2),
                    op=MULT,
                )

        def turn(rows, in_order):
            bank = turn_psum.tile([P, F // 2], F32, name="bank")
            words = rows.bitcast(F32)
            for u in range(2):
                for c in range(PASSES):
                    at = (u * PASSES + c) * P
                    cols = slice(at, at + P) if in_order else slice(2 * P * c + u, 2 * P * (c + 1), 2)
                    nc.tensor.transpose(bank[:, at : at + P], words[:, cols], ident[:])
            return bank

        def turn_run(r):
            for s in slabs_of(r, "VW") + slabs_of(r, "G"):
                bank = turn(ready[s][:], ROLES[r][s % RUN] in "GW")
                turned[s] = bank

        def grouped_half(s):
            if s // 2 not in grouped:
                t = grouped_pool.tile([P, 2 * F], BF16, name="x_grouped", align_bytes=64)
                grouped[s // 2] = t
            return grouped[s // 2][:, s % 2 * F : (s % 2 + 1) * F]

        def empty(s):
            nc.scalar.copy(
                out=grouped_half(s).bitcast(F32).rearrange("p (n u) -> p n u", u=2),
                in_=turned[s][:].rearrange("p (u n) -> p n u", u=2),
            )

        def empty_and_scale(s):
            nc.vector.tensor_tensor(
                out=grouped_half(s).rearrange("p (c r u e) -> p c r u e", c=PASSES, u=2, e=2),
                in0=turned[s][:].bitcast(BF16).rearrange("p (u c r e) -> p c r u e", u=2, c=PASSES, e=2),
                in1=scale_turned[:]
                .rearrange("p c (u e) -> p c u e", u=2)
                .unsqueeze(2)
                .to_broadcast([P, PASSES, P, 2, 2]),
                op=MULT,
            )

        def quantize(pair):
            pair_codes = code_pool.tile([P, 2 * PASSES * P], U32, name="x_codes", align_bytes=64)
            pair_scales = code_pool.tile([P, 2 * PASSES * P], U8, name="x_scales", align_bytes=64)
            nc.vector.quantize_mx(out=pair_codes[:].bitcast(FP8X4), scales=pair_scales[:], in_=grouped[pair][:])
            codes[pair], scales[pair] = pair_codes, pair_scales

        def multiply(r):
            q, i = divmod(r, BATCH_RUNS)
            if i == 0:
                t = sum_psum.tile([P, G], F32, name="sum")
                sums[q] = t
            for s in range(r * RUN, (r + 1) * RUN):
                for c in range(PASSES):
                    at = (s % 2 * PASSES + c) * P
                    nc.tensor.matmul_mx(
                        out=sums[q][:],
                        lhsT=codes[s // 2][:, at : at + P].bitcast(FP8X4),
                        lhsT_scale=scales[s // 2][:, at : at + P],
                        rhs=w1_codes[:, c, :].bitcast(FP8X4),
                        rhs_scale=w1_scales[:, c, :],
                        start=(s % SLABS == 0 and c == 0),
                        stop=(s % SLABS == SLABS - 1 and c == PASSES - 1),
                    )

        def turn_weights():
            for t in range(PACK):
                bank = turn(w1[:, t, :], False)
                nc.scalar.copy(
                    out=w1_grouped[t][:].bitcast(F32).rearrange("p c (n u) -> p c n u", u=2),
                    in_=bank[:].rearrange("p (u c n) -> p c n u", u=2, c=PASSES),
                )
            bank = turn_psum.tile([P, F // 2], F32, name="bank")
            words = w2[:].bitcast(F32)
            for u in range(2):
                nc.tensor.transpose(bank[:, u * P : (u + 1) * P], words[:, u : 2 * P : 2], ident[:])
            nc.scalar.copy(
                out=w2_grouped[:].bitcast(F32).rearrange("p (n u) -> p n u", u=2),
                in_=bank[:, : 2 * P].rearrange("p (u n) -> p n u", u=2),
            )

        def quantize_w1():
            for t in range(PACK):
                for c in range(PASSES):
                    nc.vector.quantize_mx(
                        out=w1_codes[:, c, t * P : (t + 1) * P].bitcast(FP8X4),
                        scales=w1_scales[:, c, t * P : (t + 1) * P],
                        in_=w1_grouped[t][:, c],
                    )


        def copy_sums(q):
            t = work.tile([P, G], F32, name="sums_copy")
            for i in range(2):
                part = slice(i * G // 2, (i + 1) * G // 2)
                nc.scalar.copy(out=t[:, part], in_=sums[q][:, part])
            sums_copy[q] = t

        def add_shares(q):
            t = small_psum.tile([P, G], F32, name="small")
            for i in range(PACK):
                nc.tensor.matmul(
                    t[:, i * BATCH_GRAPHS : (i + 1) * BATCH_GRAPHS],
                    lhsT=sums_copy[q][:, i * P : (i + 1) * P],
                    rhs=same_graph[:],
                    start=True,
                    stop=True,
                )
            hidden_psum[q] = t

        def mean_and_bias(q):
            t = work.tile([P, BATCH_GRAPHS, PACK], F32, name="hidden")
            nc.vector.scalar_tensor_tensor(
                out=t[:],
                in0=hidden_psum[q][:, : PACK * BATCH_GRAPHS].rearrange("p (t b) -> p b t", t=PACK),
                scalar=1.0 / NODES,
                in1=b1[:].unsqueeze(1).to_broadcast([P, BATCH_GRAPHS, PACK]),
                op0=MULT,
                op1=ADD,
            )
            hidden[q] = t

        def relu_rounded(q):
            t = work.tile([P, BATCH_GRAPHS, SHARE, PACK], BF16, name="m1", align_bytes=64)
            spread = hidden[q][:].unsqueeze(2).to_broadcast([P, BATCH_GRAPHS, SHARE, PACK])
            if q == BATCHES - 1:
                nc.vector.tensor_scalar(out=t[:], in0=spread, scalar1=0.0, scalar2=None, op0=MAX)
            else:
                nc.scalar.activation(out=t[:], in_=spread, func=RELU)
            return t

        def second_layer(q, m1):
            m1_codes = work.tile([P, P], U32, name="m1_codes", align_bytes=64)
            m1_scales = work.tile([P, P], U8, name="m1_scales", align_bytes=64)
            nc.vector.quantize_mx(
                out=m1_codes[:].bitcast(FP8X4), scales=m1_scales[:], in_=m1[:].rearrange("p b h t -> p (b h t)")
            )
            t = small_psum.tile([P, G], F32, name="small")
            nc.tensor.matmul_mx(
                out=t[:, :O],
                lhsT=m1_codes[:].bitcast(FP8X4),
                lhsT_scale=m1_scales[:],
                rhs=w2_codes[:].bitcast(FP8X4),
                rhs_scale=w2_scales[:],
                start=True,
                stop=True,
            )
            out_psum[q] = t

        def add_b2(q):
            t = work.tile([P, O], F32, name="out_sum")
            nc.vector.tensor_tensor(out=t[:], in0=out_psum[q][:, :O], in1=b2[:], op=ADD)
            out_sum[q] = t

        def store(q):
            t = work.tile([P, COPIES, O], F32, name="out_rows")
            spread = out_sum[q][:].unsqueeze(1).to_broadcast([P, COPIES, O])
            if q == BATCHES - 1:
                nc.vector.tensor_scalar(out=t[:], in0=spread, scalar1=0.0, scalar2=None, op0=MAX)
            else:
                nc.scalar.activation(out=t[:], in_=spread, func=RELU)
            nc.sync.dma_start(
                out=out_view[q].rearrange("p (a n) -> p a n", n=COPIES * O),
                in_=t[:].rearrange("p r o -> p (r o)").unsqueeze(1).to_broadcast([P, SLABS // COPIES, COPIES * O]),
            )

        load(0, RUN)
        nc.sync.dma_start(out=scale_turned[:], in_=scale_row.rearrange("(c p t) -> p c t", c=PASSES, t=PACK))
        load(1)
        for t in range(PACK):
            nc.sync.dma_start(out=w1[:, t, :], in_=w1_view[:, t, :])
        nc.sync.dma_start(out=w2[:], in_=W2g)
        nc.sync.dma_start(out=scale_plain[:], in_=scale_row.partition_broadcast(P))
        nc.sync.dma_start(out=b1[:], in_=b1g.rearrange("(p t) -> p t", t=PACK))
        nc.sync.dma_start(out=b2[:], in_=b2g.partition_broadcast(P))
        for r in range(2, LOADS):
            load(r)
        make_identity(nc, ident[:])
        nc.vector.tensor_reduce(
            out=same_graph[:],
            in_=ident[:].rearrange("p (b h) -> p b h", h=SHARE),
            axis=mybir.AxisListType.X,
            op=ADD,
        )

        with tc.manual_schedule():
            for r in range(RUNS + 3):
                live = r < RUNS
                by_vector = slabs_of(r, "VW") if live else []
                pairs = [r * RUN // 2 + i for i in range(RUN // 2)] if live else []
                summed, shared, finished = [
                    (r - d) // BATCH_RUNS if r >= d and (r - d) % BATCH_RUNS == BATCH_RUNS - 1 else None
                    for d in (1, 2, 3)
                ]

                if r == 0:
                    widen(0, "V")
                if r + LOADS < RUNS:
                    load(r + LOADS)
                if live:
                    turn_run(r)
                    for s in slabs_of(r, "G"):
                        empty(s)
                if r == 0:
                    widen(1, "WV")
                    turn_weights()
                for s in by_vector[:1]:
                    empty_and_scale(s)
                if finished is not None:
                    m1 = relu_rounded(finished)
                for s in by_vector[1:2]:
                    empty_and_scale(s)
                if r == 1:
                    quantize_w1()
                    hold_gpsimd(2)
                    scale_on_gpsimd(2)
                if 1 <= r <= RUNS:
                    multiply(r - 1)
                if shared is not None:
                    add_shares(shared)
                if finished is not None:
                    second_layer(finished, m1)
                if r == RUNS - 1:
                    quantize(pairs[0])
                for s in by_vector[2:]:
                    empty_and_scale(s)
                if r == 0:
                    nc.vector.tensor_copy(
                        out=scale_sorted[:].rearrange("p (u n e) -> p u n e", u=2, e=2),
                        in_=scale_plain[:].rearrange("p (n u e) -> p u n e", u=2, e=2),
                    )
                if r == 2:
                    nc.vector.quantize_mx(out=w2_codes[:].bitcast(FP8X4), scales=w2_scales[:], in_=w2_grouped[:])
                if r < RUNS - 1:
                    quantize(pairs[0])
                if 1 <= r < RUNS - 2:
                    hold_gpsimd(r + 2)
                if live:
                    quantize(pairs[1])
                if shared is not None:
                    mean_and_bias(shared)
                if finished is not None:
                    add_b2(finished)
                if 1 <= r < RUNS - 2:
                    scale_on_gpsimd(r + 2)
                for n in [2, 3] if r == 0 else [r + 3]:
                    if n < RUNS:
                        widen(n, "G")
                if r + 2 < RUNS:
                    widen(r + 2, "WV")
                if summed is not None:
                    copy_sums(summed)
                if finished is not None:
                    store(finished)
